import numpy as np
import ml_dtypes


def mxq(x, axis, fmt="e4m3"):
    dtype, down = {"e4m3": (ml_dtypes.float8_e4m3fn, 7), "e5m2": (ml_dtypes.float8_e5m2, 14)}[fmt]
    v = np.moveaxis(np.asarray(x, np.float32).astype(ml_dtypes.bfloat16).astype(np.float64), axis, -1)
    blocks = v.reshape(v.shape[:-1] + (-1, 32))
    amax = np.abs(blocks).max(-1, keepdims=True)
    byte = np.maximum(np.where(amax > 0, np.frexp(amax)[1] - 1 + 127, 0) - down, 1)
    scale = np.exp2(byte - 127.0)
    codes = (blocks / scale).astype(np.float32).astype(dtype).astype(np.float64)
    return np.moveaxis((codes * scale).reshape(v.shape), -1, axis)


WIDE = False


def mx_kscale(k):
    if not WIDE:
        return np.ones(k)
    levels = np.array([10, -10, 5, -5, 0])
    a = np.random.permutation(np.resize(levels, k // 512 * 4)).reshape(k // 512, 4)
    idx = np.arange(k)
    return np.exp2(a[idx // 512, idx % 128 // 32])


BF16 = ml_dtypes.bfloat16


def bf(x):
    return np.asarray(x, np.float32).astype(BF16)


def f64(x):
    return np.asarray(x).astype(np.float64)


E2M1 = np.array([0.0, 0.5, 1.0, 1.5, 2.0, 3.0, 4.0, 6.0, -0.0, -0.5, -1.0, -1.5, -2.0, -3.0, -4.0, -6.0])


def pack_weight(w, fmt):
    k, n = w.shape
    w = f64(bf(w)).reshape(k // 32, 32, n)
    amax = np.abs(w).max(1)
    if fmt == "e4m3":
        byte = np.frexp(amax)[1] - 1 + 127 - 7
    else:
        mant, ex = np.frexp(amax / 6.0)
        byte = np.where(mant > 0.5, ex, ex - 1) + 127
    byte = np.clip(np.where(amax > 0, byte, 1), 1, 254)
    scaled = (w * np.exp2(127.0 - byte)[:, None, :]).reshape(k, n).astype(np.float32)
    by_word = np.ascontiguousarray(scaled.reshape(k // 512, 128, 4, n).transpose(0, 1, 3, 2))
    if fmt == "e4m3":
        words = by_word.astype(ml_dtypes.float8_e4m3fn).view(np.uint8)
    else:
        c = by_word.astype(ml_dtypes.float4_e2m1fn).view(np.uint8) & 0xF
        words = c[..., 0::2] | (c[..., 1::2] << 4)
    return np.ascontiguousarray(words), np.ascontiguousarray(byte.astype(np.uint8).reshape(k // 512, 16, n))


def unpack_weight(words, scales, fmt):
    g, p, n, _ = words.shape
    if fmt == "e4m3":
        vals = np.ascontiguousarray(words).view(ml_dtypes.float8_e4m3fn).astype(np.float64)
    else:
        nib = np.empty((g, p, n, 4), np.uint8)
        nib[..., 0::2] = words & 0xF
        nib[..., 1::2] = words >> 4
        vals = E2M1[nib]
    vals = vals * np.repeat(np.exp2(scales.astype(np.float64) - 127.0), 8, axis=1)[..., None]
    return vals.transpose(0, 1, 3, 2).reshape(g * 512, n)


B, I, N, L = 512, 512, 1024, 2
SIGSIZE = sum(2 ** k for k in range(1, L + 1))
SAVED = N * (1 + SIGSIZE)


def sigjoin(prev_sigs, disp, time_lapse, level):
    n = prev_sigs.shape[0]
    v = np.concatenate([disp, np.full_like(disp, 1.0) * time_lapse], axis=1)
    seg = [v]
    for k in range(2, level + 1):
        seg.append((seg[-1][:, :, None] * v[:, None, :]).reshape(n, -1) / k)
    S, off = [], 0
    for k in range(1, level + 1):
        sz = 2 ** k
        S.append(prev_sigs[:, off:off + sz])
        off += sz
    out = []
    for k in range(1, level + 1):
        r = S[k - 1] + seg[k - 1]
        for i in range(1, k):
            r = r + (S[i - 1][:, :, None] * seg[k - i - 1][:, None, :]).reshape(n, 2 ** k)
        out.append(r)
    return np.concatenate(out, axis=1)


def setup_inputs():
    s = mx_kscale(I)
    u = mx_kscale(SAVED)
    d = np.minimum(u, 1.0 / u) ** 2
    x = bf(np.random.standard_normal((B, I)) * s)
    prev_sigs = bf(np.random.standard_normal((B, N * SIGSIZE)) * 0.5 * d[:N * SIGSIZE])
    prev_states = bf(np.random.standard_normal((B, N)) * d[N * SIGSIZE:])
    W_w_words, W_w_scales = pack_weight(np.ascontiguousarray((np.random.standard_normal((N, I)) / np.sqrt(I) / s).T), "e4m3")
    W_b = bf(np.random.standard_normal(N) * 0.1)
    U_w_words, U_w_scales = pack_weight(np.ascontiguousarray((np.random.standard_normal((N, SAVED)) / np.sqrt(SAVED) / d).T), "e4m3")
    U_b = bf(np.random.standard_normal(N) * 0.1)
    log_timelapse = bf(np.log(0.1) + 0.2 * np.random.standard_normal(1))
    return {"x": x,
            "prev_sigs": prev_sigs,
            "prev_states": prev_states,
            "W_w_words": W_w_words,
            "W_w_scales": W_w_scales,
            "W_b": W_b,
            "U_w_words": U_w_words,
            "U_w_scales": U_w_scales,
            "U_b": U_b,
            "log_timelapse": log_timelapse}


def reference(x, prev_sigs, prev_states, W_w_words, W_w_scales, W_b, U_w_words, U_w_scales, U_b, log_timelapse):
    h = (mxq(f64(x), 1, "e4m3") @ unpack_weight(W_w_words, W_w_scales, "e4m3")) + f64(W_b)
    mem = np.concatenate([f64(prev_sigs), f64(prev_states)], 1)
    raw = h + (mxq(mem, 1, "e4m3") @ unpack_weight(U_w_words, U_w_scales, "e4m3")) + f64(U_b)
    disp = (raw - f64(prev_states)).reshape(-1, 1)
    tl = np.exp(f64(log_timelapse))[0]
    sigs = sigjoin(f64(prev_sigs).reshape(-1, SIGSIZE), disp, tl, L)
    sigs = sigs.reshape(-1, N * SIGSIZE)
    return np.concatenate([sigs, raw], axis=1)

@@ -1,0 +1,257 @@
+from contextlib import ExitStack
+
+import concourse.mybir as mybir
+from concourse.masks import make_identity
+
+F32 = mybir.dt.float32
+BF16 = mybir.dt.bfloat16
+I32 = mybir.dt.int32
+U32 = mybir.dt.uint32
+U8 = mybir.dt.uint8
+FP8X4 = mybir.dt.float8_e4m3fn_x4
+ALU = mybir.AluOpType
+FUNC = mybir.ActivationFunctionType
+
+P = 128
+BATCH = 512
+INPUTS = 512
+UNITS = 1024
+SIG = 6
+SIG_COLS = UNITS * SIG
+K_PASS = 512
+K_ALL = SIG_COLS + UNITS + INPUTS
+GROUPS = K_ALL // K_PASS
+U_GROUPS = (SIG_COLS + UNITS) // K_PASS
+WORDS = K_PASS // 2
+TILES = BATCH // P
+HALF = 512
+HALVES = UNITS // HALF
+ROUND = 2
+RUN = 4
+PLANES_PER_SLOT = 4
+PIECE = 256
+PAIR = 2
+ACT_BUFS = 3
+AHEAD = 2
+
+FLOPS = 2 * BATCH * K_ALL * UNITS
+
+
+def tile_recurrentsig_kernel(
+    tc,
+    x,
+    prev_sigs,
+    prev_states,
+    W_w_words,
+    W_w_scales,
+    W_b,
+    U_w_words,
+    U_w_scales,
+    U_b,
+    log_timelapse,
+    out,
+):
+    nc = tc.nc
+    with ExitStack() as ctx:
+        const = ctx.enter_context(tc.tile_pool(name="const", bufs=1))
+        acts = ctx.enter_context(tc.tile_pool(name="acts", bufs=ACT_BUFS))
+        quant = ctx.enter_context(tc.tile_pool(name="quant", bufs=2))
+        stage = ctx.enter_context(tc.tile_pool(name="stage", bufs=4))
+        small = ctx.enter_context(tc.tile_pool(name="small", bufs=2))
+        raws = ctx.enter_context(tc.tile_pool(name="raws", bufs=3))
+        joins = ctx.enter_context(tc.tile_pool(name="joins", bufs=6))
+        psum_t = ctx.enter_context(tc.psum_pool(name="psum_t", bufs=4))
+        psum_acc = ctx.enter_context(tc.psum_pool(name="psum_acc", bufs=4))
+
+        w_words = const.tile([P, GROUPS, UNITS], U32, align_bytes=64)
+        w_planes = const.tile([P, PLANES_PER_SLOT, UNITS], U8, align_bytes=64)
+        nc.vector.memset(w_planes[:].bitcast(I32), 0)
+
+        ident = const.tile([P, P], F32)
+        make_identity(nc, ident[:])
+
+        bias_rows = const.tile([P, UNITS], BF16)
+        nc.vector.memset(bias_rows[:], 0.0)
+        ones = const.tile([P, P], BF16)
+        nc.vector.memset(ones[:], 1.0)
+        nc.scalar.dma_start(out=bias_rows[0:1, :], in_=W_b.unsqueeze(0))
+        nc.scalar.dma_start(out=bias_rows[1:2, :], in_=U_b.unsqueeze(0))
+        log_tl = const.tile([P, 1], BF16)
+        nc.scalar.dma_start(out=log_tl[:], in_=log_timelapse.partition_broadcast(P))
+
+        act = {}
+
+        def load_activations(bt, after_piece):
+            rows = slice(bt * P, (bt + 1) * P)
+            tile_bt = acts.tile([P, K_ALL], BF16, tag="act", name="act%d" % bt)
+            act[bt] = tile_bt
+            piece_cols = RUN * K_PASS
+            for i in range(SIG_COLS // piece_cols):
+                cols = slice(i * piece_cols, (i + 1) * piece_cols)
+                nc.sync.dma_start(out=tile_bt[:, cols], in_=prev_sigs[rows, cols])
+                after_piece(i)
+            nc.sync.dma_start(out=tile_bt[:, SIG_COLS : SIG_COLS + UNITS], in_=prev_states[rows, :])
+            nc.sync.dma_start(out=tile_bt[:, SIG_COLS + UNITS : K_ALL], in_=x[rows, :])
+
+        def load_scale_slot(slot):
+            first = slot * PLANES_PER_SLOT
+            last = min(first + PLANES_PER_SLOT, U_GROUPS)
+            for quadrant in range(4):
+                top = 32 * quadrant
+                rows = slice(4 * quadrant, 4 * quadrant + 4)
+                nc.sync.dma_start(
+                    out=w_planes[top : top + 4 * (last - first), slot, :].bitcast(I32),
+                    in_=U_w_scales[first:last, rows, :].bitcast(I32),
+                )
+                if last == U_GROUPS:
+                    top_w = top + 4 * (U_GROUPS - first)
+                    nc.sync.dma_start(
+                        out=w_planes[top_w : top_w + 4, slot, :].bitcast(I32),
+                        in_=W_w_scales[0, rows, :].bitcast(I32),
+                    )
+
+        def load_weight_words(half):
+            cols = slice(half * HALF, (half + 1) * HALF)
+            for first in range(0, U_GROUPS, RUN):
+                last = min(first + RUN, U_GROUPS)
+                nc.sync.dma_start(
+                    out=w_words[:, first:last, cols].bitcast(I32),
+                    in_=U_w_words[first:last, :, cols, :].rearrange("g p n t -> p g (n t)").bitcast(I32),
+                )
+            nc.sync.dma_start(
+                out=w_words[:, U_GROUPS, cols].bitcast(I32),
+                in_=W_w_words[0, :, cols, :].rearrange("p n t -> p (n t)").bitcast(I32),
+            )
+
+        def nothing(i):
+            return None
+
+        load_activations(0, load_scale_slot)
+        load_scale_slot(PLANES_PER_SLOT - 1)
+        load_weight_words(0)
+        load_activations(1, nothing)
+        load_weight_words(1)
+        load_activations(2, nothing)
+
+        tl = const.tile([P, 1], F32)
+        nc.scalar.activation(out=tl[:], in_=log_tl[:], func=FUNC.Exp)
+        half_tl = const.tile([P, 1], F32)
+        nc.scalar.mul(out=half_tl[:], in_=tl[:], mul=0.5)
+
+        bias = const.tile([P, UNITS], F32)
+        for half in range(HALVES):
+            cols = slice(half * HALF, (half + 1) * HALF)
+            bias_ps = psum_acc.tile([P, HALF], F32, tag="acc")
+            nc.tensor.matmul(out=bias_ps[:], lhsT=ones[:], rhs=bias_rows[:, cols], start=True, stop=True)
+            nc.vector.tensor_copy(out=bias[:, cols], in_=bias_ps[:])
+
+        plane_sets = []
+        for s in range(2):
+            planes = const.tile([P, SIG, HALF], F32, name="planes%d" % s)
+            nc.vector.tensor_copy(out=planes[:, 1, :], in_=tl[:, 0:1].to_broadcast([P, HALF]))
+            plane_sets.append(planes)
+
+        a_words = {}
+        a_scales = {}
+
+        def transpose_and_quantise(bt, first):
+            count = min(ROUND, GROUPS - first)
+            words = act[bt][:].bitcast(F32)
+            turned = psum_t.tile([P, ROUND, 2, P], F32, tag="turned")
+            for i in range(count):
+                g = first + i
+                for u in range(2):
+                    nc.tensor.transpose(
+                        turned[:, i, u, :], words[:, WORDS * g + u : WORDS * (g + 1) : 2], ident[:]
+                    )
+            grouped = stage.tile([P, ROUND * K_PASS], BF16, align_bytes=64)
+            nc.scalar.copy(
+                out=grouped[:, 0 : count * K_PASS].bitcast(F32).rearrange("p (g b u) -> p g b u", g=count, u=2),
+                in_=turned[:, 0:count].rearrange("p g u b -> p g b u"),
+            )
+            nc.vector.quantize_mx(
+                out=a_words[bt][:, first : first + count, :].rearrange("p g b -> p (g b)").bitcast(FP8X4),
+                scales=a_scales[bt][:, first : first + count, :].rearrange("p g b -> p (g b)"),
+                in_=grouped[:, 0 : count * K_PASS],
+            )
+
+        def passes(bt, half, acc, groups):
+            cols = slice(half * HALF, (half + 1) * HALF)
+            for g in groups:
+                nc.tensor.matmul_mx(
+                    out=acc[:],
+                    lhsT=a_words[bt][:, g, :].bitcast(FP8X4),
+                    lhsT_scale=a_scales[bt][:, g, :],
+                    rhs=w_words[:, g, cols].bitcast(FP8X4),
+                    rhs_scale=w_planes[4 * (g % PLANES_PER_SLOT) : P, g // PLANES_PER_SLOT, cols],
+                    start=(g == 0),
+                    stop=(g == GROUPS - 1),
+                )
+
+        def tensor_work(bt, half, acc):
+            if half > 0:
+                passes(bt, half, acc, range(GROUPS))
+                return
+            a_words[bt] = quant.tile([P, GROUPS, P], U32, align_bytes=64, tag="a_words", name="a_words%d" % bt)
+            a_scales[bt] = quant.tile([P, GROUPS, P], U8, align_bytes=64, tag="a_scales", name="a_scales%d" % bt)
+            for run in range(0, GROUPS, RUN):
+                for first in range(run, min(run + RUN, GROUPS), ROUND):
+                    transpose_and_quantise(bt, first)
+                if run > 0:
+                    passes(bt, half, acc, range(run - RUN, run))
+            passes(bt, half, acc, range(GROUPS - GROUPS % RUN, GROUPS))
+
+        def epilogue(bt, half, acc, planes):
+            rows = slice(bt * P, (bt + 1) * P)
+            units = slice(half * HALF, (half + 1) * HALF)
+            sigs = act[bt][:, half * HALF * SIG : (half + 1) * HALF * SIG]
+            by_unit = sigs.rearrange("p (n j) -> p n j", j=SIG)
+            states = act[bt][:, SIG_COLS + half * HALF : SIG_COLS + (half + 1) * HALF]
+
+            a0 = small.tile([P, HALF], BF16)
+            nc.scalar.copy(out=a0[:], in_=by_unit[:, :, 0])
+            c = small.tile([P, 2, HALF], F32)
+            nc.scalar.activation(
+                out=c[:, 1, :], in_=by_unit[:, :, 1], func=FUNC.Identity, bias=half_tl[:, 0:1], scale=1.0
+            )
+
+            raw = raws.tile([P, HALF], F32)
+            nc.vector.tensor_tensor(out=raw[:], in0=acc[:], in1=bias[:, units], op=ALU.add)
+            nc.vector.tensor_tensor(out=planes[:, 0, :], in0=raw[:], in1=states, op=ALU.subtract)
+            nc.vector.scalar_tensor_tensor(
+                out=c[:, 0, :], in0=planes[:, 0, :], scalar=0.5, in1=a0[:], op0=ALU.mult, op1=ALU.add
+            )
+            nc.vector.tensor_tensor(
+                out=planes[:, 2:5:2, :], in0=c[:], in1=planes[:, 0:1, :].to_broadcast([P, 2, HALF]), op=ALU.mult
+            )
+            nc.scalar.activation(out=planes[:, 3:6:2, :], in_=c[:], func=FUNC.Copy, scale=tl[:, 0:1])
+            nc.sync.dma_start(out=out[rows, SIG_COLS + half * HALF : SIG_COLS + (half + 1) * HALF], in_=raw[:])
+
+            for n0 in range(0, HALF, PIECE):
+                joined = joins.tile([P, PIECE * SIG], F32)
+                nc.vector.tensor_tensor(
+                    out=joined[:].rearrange("p (m r j) -> p m j r", r=PAIR, j=SIG),
+                    in0=planes[:, :, n0 : n0 + PIECE].rearrange("p j (m r) -> p m j r", r=PAIR),
+                    in1=sigs[:, n0 * SIG : (n0 + PIECE) * SIG].rearrange("p (m r j) -> p m j r", r=PAIR, j=SIG),
+                    op=ALU.add,
+                )
+                first_col = (half * HALF + n0) * SIG
+                nc.sync.dma_start(out=out[rows, first_col : first_col + PIECE * SIG], in_=joined[:])
+
+        cells = [(bt, half) for pair in range(0, TILES, 2) for half in range(HALVES) for bt in (pair, pair + 1)]
+        accs = {}
+
+        def start_cell(i):
+            bt, half = cells[i]
+            accs[i] = psum_acc.tile([P, HALF], F32, tag="acc", name="acc%d" % i)
+            tensor_work(bt, half, accs[i])
+
+        for i in range(AHEAD):
+            start_cell(i)
+        for i in range(len(cells)):
+            if i + AHEAD < len(cells):
+                start_cell(i + AHEAD)
+            bt, half = cells[i]
+            epilogue(bt, half, accs[i], plane_sets[i % 2])
+            if half == HALVES - 1 and bt + ACT_BUFS < TILES:
+                load_activations(bt + ACT_BUFS, nothing)

@@ -17,22 +17,25 @@ BATCH = 512
 INPUTS = 512
 UNITS = 1024
 SIG = 6
-SIG_COLS = UNITS * SIG
 K_PASS = 512
-K_ALL = SIG_COLS + UNITS + INPUTS
+K_ALL = UNITS * SIG + UNITS + INPUTS
 GROUPS = K_ALL // K_PASS
-U_GROUPS = (SIG_COLS + UNITS) // K_PASS
+U_GROUPS = GROUPS - INPUTS // K_PASS
 WORDS = K_PASS // 2
 TILES = BATCH // P
 HALF = 512
 HALVES = UNITS // HALF
+SIG_GROUPS = HALF * SIG // K_PASS
 ROUND = 2
-RUN = 4
+RUN = SIG_GROUPS
+RUNS = -(-GROUPS // RUN)
 PLANES_PER_SLOT = 4
-PIECE = 256
+PIECE = 128
 PAIR = 2
-ACT_BUFS = 3
-AHEAD = 2
+STORE = 2 * PIECE
+LOADED_FIRST = 3
+STEPS = RUNS + 1
+assert HALF // PIECE == STEPS
 
 FLOPS = 2 * BATCH * K_ALL * UNITS
 
@@ -53,8 +56,10 @@ def tile_recurrentsig_kernel(
 ):
     nc = tc.nc
     with ExitStack() as ctx:
+        ctx.enter_context(tc.manual_schedule())
         const = ctx.enter_context(tc.tile_pool(name="const", bufs=1))
-        acts = ctx.enter_context(tc.tile_pool(name="acts", bufs=ACT_BUFS))
+        sig_pool = ctx.enter_context(tc.tile_pool(name="sig_pool", bufs=LOADED_FIRST * HALVES))
+        rest_pool = ctx.enter_context(tc.tile_pool(name="rest_pool", bufs=TILES))
         quant = ctx.enter_context(tc.tile_pool(name="quant", bufs=2))
         stage = ctx.enter_context(tc.tile_pool(name="stage", bufs=4))
         small = ctx.enter_context(tc.tile_pool(name="small", bufs=2))
@@ -79,19 +84,22 @@ def tile_recurrentsig_kernel(
         log_tl = const.tile([P, 1], BF16)
         nc.scalar.dma_start(out=log_tl[:], in_=log_timelapse.partition_broadcast(P))
 
-        act = {}
+        sig_tiles = {}
+        rest_tiles = {}
 
-        def load_activations(bt, after_piece):
+        def load_activations(bt, behind_each_load):
             rows = slice(bt * P, (bt + 1) * P)
-            tile_bt = acts.tile([P, K_ALL], BF16, tag="act", name="act%d" % bt)
-            act[bt] = tile_bt
-            piece_cols = RUN * K_PASS
-            for i in range(SIG_COLS // piece_cols):
-                cols = slice(i * piece_cols, (i + 1) * piece_cols)
-                nc.sync.dma_start(out=tile_bt[:, cols], in_=prev_sigs[rows, cols])
-                after_piece(i)
-            nc.sync.dma_start(out=tile_bt[:, SIG_COLS : SIG_COLS + UNITS], in_=prev_states[rows, :])
-            nc.sync.dma_start(out=tile_bt[:, SIG_COLS + UNITS : K_ALL], in_=x[rows, :])
+            for half in range(HALVES):
+                sigs = sig_pool.tile([P, HALF * SIG], BF16, tag="sigs", name="sigs%d_%d" % (bt, half))
+                sig_tiles[bt, half] = sigs
+                nc.sync.dma_start(out=sigs[:], in_=prev_sigs[rows, half * HALF * SIG : (half + 1) * HALF * SIG])
+                behind_each_load(half)
+            rest = rest_pool.tile([P, UNITS + INPUTS], BF16, tag="rest", name="rest%d" % bt)
+            rest_tiles[bt] = rest
+            nc.sync.dma_start(out=rest[:, 0:UNITS], in_=prev_states[rows, :])
+            behind_each_load(HALVES)
+            nc.sync.dma_start(out=rest[:, UNITS : UNITS + INPUTS], in_=x[rows, :])
+            behind_each_load(HALVES + 1)
 
         def load_scale_slot(slot):
             first = slot * PLANES_PER_SLOT
@@ -127,7 +135,6 @@ def tile_recurrentsig_kernel(
             return None
 
         load_activations(0, load_scale_slot)
-        load_scale_slot(PLANES_PER_SLOT - 1)
         load_weight_words(0)
         load_activations(1, nothing)
         load_weight_words(1)
@@ -145,25 +152,22 @@ def tile_recurrentsig_kernel(
             nc.tensor.matmul(out=bias_ps[:], lhsT=ones[:], rhs=bias_rows[:, cols], start=True, stop=True)
             nc.vector.tensor_copy(out=bias[:, cols], in_=bias_ps[:])
 
-        plane_sets = []
-        for s in range(2):
-            planes = const.tile([P, SIG, HALF], F32, name="planes%d" % s)
-            nc.vector.tensor_copy(out=planes[:, 1, :], in_=tl[:, 0:1].to_broadcast([P, HALF]))
-            plane_sets.append(planes)
-
         a_words = {}
         a_scales = {}
 
-        def transpose_and_quantise(bt, first):
-            count = min(ROUND, GROUPS - first)
-            words = act[bt][:].bitcast(F32)
+        def group_words(bt, g):
+            if g < HALVES * SIG_GROUPS:
+                source, local = sig_tiles[bt, g // SIG_GROUPS], g % SIG_GROUPS
+            else:
+                source, local = rest_tiles[bt], g - HALVES * SIG_GROUPS
+            return source[:, local * K_PASS : (local + 1) * K_PASS].bitcast(F32)
+
+        def transpose_and_quantise(bt, first, count):
             turned = psum_t.tile([P, ROUND, 2, P], F32, tag="turned")
             for i in range(count):
-                g = first + i
+                words = group_words(bt, first + i)
                 for u in range(2):
-                    nc.tensor.transpose(
-                        turned[:, i, u, :], words[:, WORDS * g + u : WORDS * (g + 1) : 2], ident[:]
-                    )
+                    nc.tensor.transpose(turned[:, i, u, :], words[:, u:WORDS:2], ident[:])
             grouped = stage.tile([P, ROUND * K_PASS], BF16, align_bytes=64)
             nc.scalar.copy(
                 out=grouped[:, 0 : count * K_PASS].bitcast(F32).rearrange("p (g b u) -> p g b u", g=count, u=2),
@@ -175,83 +179,104 @@ def tile_recurrentsig_kernel(
                 in_=grouped[:, 0 : count * K_PASS],
             )
 
-        def passes(bt, half, acc, groups):
+        def tensor_part(i, part):
+            bt, half = cells[i]
             cols = slice(half * HALF, (half + 1) * HALF)
-            for g in groups:
-                nc.tensor.matmul_mx(
-                    out=acc[:],
-                    lhsT=a_words[bt][:, g, :].bitcast(FP8X4),
-                    lhsT_scale=a_scales[bt][:, g, :],
-                    rhs=w_words[:, g, cols].bitcast(FP8X4),
-                    rhs_scale=w_planes[4 * (g % PLANES_PER_SLOT) : P, g // PLANES_PER_SLOT, cols],
-                    start=(g == 0),
-                    stop=(g == GROUPS - 1),
+            if part == 0:
+                accs[i] = psum_acc.tile([P, HALF], F32, tag="acc", name="acc%d" % i)
+            if part == 0 and half == 0:
+                a_words[bt] = quant.tile([P, GROUPS, P], U32, align_bytes=64, tag="a_words", name="a_words%d" % bt)
+                a_scales[bt] = quant.tile([P, GROUPS, P], U8, align_bytes=64, tag="a_scales", name="a_scales%d" % bt)
+            if part < RUNS and half == 0:
+                end = min((part + 1) * RUN, GROUPS)
+                for first in range(part * RUN, end, ROUND):
+                    transpose_and_quantise(bt, first, min(ROUND, end - first))
+            if part > 0:
+                for g in range((part - 1) * RUN, min(part * RUN, GROUPS)):
+                    nc.tensor.matmul_mx(
+                        out=accs[i][:],
+                        lhsT=a_words[bt][:, g, :].bitcast(FP8X4),
+                        lhsT_scale=a_scales[bt][:, g, :],
+                        rhs=w_words[:, g, cols].bitcast(FP8X4),
+                        rhs_scale=w_planes[4 * (g % PLANES_PER_SLOT) : P, g // PLANES_PER_SLOT, cols],
+                        start=(g == 0),
+                        stop=(g == GROUPS - 1),
+                    )
+
+        plane_sets = [const.tile([P, SIG, HALF], F32, name="planes%d" % s) for s in range(2)]
+
+        cell_tiles = {}
+
+        def plane_step(i, step):
+            bt, half = cells[i]
+            planes = plane_sets[i % 2]
+            if step == 0:
+                by_unit = sig_tiles[bt, half][:].rearrange("p (n j) -> p n j", j=SIG)
+                a0 = small.tile([P, HALF], BF16)
+                nc.scalar.copy(out=a0[:], in_=by_unit[:, :, 0])
+                c = small.tile([P, 2, HALF], F32)
+                nc.scalar.activation(
+                    out=c[:, 1, :], in_=by_unit[:, :, 1], func=FUNC.Identity, bias=half_tl[:, 0:1], scale=1.0
                 )
-
-        def tensor_work(bt, half, acc):
-            if half > 0:
-                passes(bt, half, acc, range(GROUPS))
-                return
-            a_words[bt] = quant.tile([P, GROUPS, P], U32, align_bytes=64, tag="a_words", name="a_words%d" % bt)
-            a_scales[bt] = quant.tile([P, GROUPS, P], U8, align_bytes=64, tag="a_scales", name="a_scales%d" % bt)
-            for run in range(0, GROUPS, RUN):
-                for first in range(run, min(run + RUN, GROUPS), ROUND):
-                    transpose_and_quantise(bt, first)
-                if run > 0:
-                    passes(bt, half, acc, range(run - RUN, run))
-            passes(bt, half, acc, range(GROUPS - GROUPS % RUN, GROUPS))
-
-        def epilogue(bt, half, acc, planes):
-            rows = slice(bt * P, (bt + 1) * P)
-            units = slice(half * HALF, (half + 1) * HALF)
-            sigs = act[bt][:, half * HALF * SIG : (half + 1) * HALF * SIG]
-            by_unit = sigs.rearrange("p (n j) -> p n j", j=SIG)
-            states = act[bt][:, SIG_COLS + half * HALF : SIG_COLS + (half + 1) * HALF]
-
-            a0 = small.tile([P, HALF], BF16)
-            nc.scalar.copy(out=a0[:], in_=by_unit[:, :, 0])
-            c = small.tile([P, 2, HALF], F32)
-            nc.scalar.activation(
-                out=c[:, 1, :], in_=by_unit[:, :, 1], func=FUNC.Identity, bias=half_tl[:, 0:1], scale=1.0
-            )
-
-            raw = raws.tile([P, HALF], F32)
-            nc.vector.tensor_tensor(out=raw[:], in0=acc[:], in1=bias[:, units], op=ALU.add)
-            nc.vector.tensor_tensor(out=planes[:, 0, :], in0=raw[:], in1=states, op=ALU.subtract)
-            nc.vector.scalar_tensor_tensor(
-                out=c[:, 0, :], in0=planes[:, 0, :], scalar=0.5, in1=a0[:], op0=ALU.mult, op1=ALU.add
-            )
-            nc.vector.tensor_tensor(
-                out=planes[:, 2:5:2, :], in0=c[:], in1=planes[:, 0:1, :].to_broadcast([P, 2, HALF]), op=ALU.mult
-            )
-            nc.scalar.activation(out=planes[:, 3:6:2, :], in_=c[:], func=FUNC.Copy, scale=tl[:, 0:1])
-            nc.sync.dma_start(out=out[rows, SIG_COLS + half * HALF : SIG_COLS + (half + 1) * HALF], in_=raw[:])
-
-            for n0 in range(0, HALF, PIECE):
-                joined = joins.tile([P, PIECE * SIG], F32)
+                raw = raws.tile([P, HALF], F32)
+                cell_tiles[i] = (a0, c, raw)
                 nc.vector.tensor_tensor(
-                    out=joined[:].rearrange("p (m r j) -> p m j r", r=PAIR, j=SIG),
-                    in0=planes[:, :, n0 : n0 + PIECE].rearrange("p j (m r) -> p m j r", r=PAIR),
-                    in1=sigs[:, n0 * SIG : (n0 + PIECE) * SIG].rearrange("p (m r j) -> p m j r", r=PAIR, j=SIG),
-                    op=ALU.add,
+                    out=raw[:], in0=accs[i][:], in1=bias[:, half * HALF : (half + 1) * HALF], op=ALU.add
                 )
-                first_col = (half * HALF + n0) * SIG
-                nc.sync.dma_start(out=out[rows, first_col : first_col + PIECE * SIG], in_=joined[:])
+                first_col = UNITS * SIG + half * HALF
+                nc.sync.dma_start(out=out[bt * P : (bt + 1) * P, first_col : first_col + HALF], in_=raw[:])
+            a0, c, raw = cell_tiles[i]
+            if step == 1:
+                states = rest_tiles[bt][:, half * HALF : (half + 1) * HALF]
+                nc.vector.tensor_tensor(out=planes[:, 0, :], in0=raw[:], in1=states, op=ALU.subtract)
+            if step == 2:
+                nc.vector.scalar_tensor_tensor(
+                    out=c[:, 0, :], in0=planes[:, 0, :], scalar=0.5, in1=a0[:], op0=ALU.mult, op1=ALU.add
+                )
+                nc.scalar.activation(out=planes[:, 3:6:2, :], in_=c[:], func=FUNC.Copy, scale=tl[:, 0:1])
+            if step == 3:
+                nc.vector.tensor_tensor(
+                    out=planes[:, 2:5:2, :], in0=c[:], in1=planes[:, 0:1, :].to_broadcast([P, 2, HALF]), op=ALU.mult
+                )
+
+        joined_tiles = {}
+
+        def join_piece(i, piece):
+            bt, half = cells[i]
+            n0 = piece * PIECE
+            if n0 % STORE == 0:
+                joined_tiles[i] = joins.tile([P, STORE * SIG], F32, tag="joined", name="joined%d_%d" % (i, piece))
+            joined = joined_tiles[i]
+            nc.vector.tensor_tensor(
+                out=joined[:, (n0 % STORE) * SIG : (n0 % STORE + PIECE) * SIG].rearrange(
+                    "p (m r j) -> p m j r", r=PAIR, j=SIG
+                ),
+                in0=plane_sets[i % 2][:, :, n0 : n0 + PIECE].rearrange("p j (m r) -> p m j r", r=PAIR),
+                in1=sig_tiles[bt, half][:, n0 * SIG : (n0 + PIECE) * SIG].rearrange(
+                    "p (m r j) -> p m j r", r=PAIR, j=SIG
+                ),
+                op=ALU.add,
+            )
+            if (n0 + PIECE) % STORE == 0:
+                first_col = (half * HALF + n0 + PIECE - STORE) * SIG
+                nc.sync.dma_start(out=out[bt * P : (bt + 1) * P, first_col : first_col + STORE * SIG], in_=joined[:])
 
         cells = [(bt, half) for pair in range(0, TILES, 2) for half in range(HALVES) for bt in (pair, pair + 1)]
         accs = {}
 
-        def start_cell(i):
-            bt, half = cells[i]
-            accs[i] = psum_acc.tile([P, HALF], F32, tag="acc", name="acc%d" % i)
-            tensor_work(bt, half, accs[i])
-
-        for i in range(AHEAD):
-            start_cell(i)
-        for i in range(len(cells)):
-            if i + AHEAD < len(cells):
-                start_cell(i + AHEAD)
-            bt, half = cells[i]
-            epilogue(bt, half, accs[i], plane_sets[i % 2])
-            if half == HALVES - 1 and bt + ACT_BUFS < TILES:
-                load_activations(bt + ACT_BUFS, nothing)
+        for part in range(STEPS):
+            tensor_part(0, part)
+        for planes in plane_sets:
+            nc.vector.tensor_copy(out=planes[:, 1, :], in_=tl[:, 0:1].to_broadcast([P, HALF]))
+        for i in range(-1, len(cells)):
+            for step in range(STEPS):
+                if i + 2 < len(cells):
+                    tensor_part(i + 2, step)
+                if i + 1 < len(cells):
+                    plane_step(i + 1, step)
+                if i >= 0:
+                    join_piece(i, step)
+            if i >= 0:
+                bt, half = cells[i]
+                if half == 0 and bt % 2 == 1 and LOADED_FIRST <= bt + 2 < TILES:
+                    load_activations(bt + 2, nothing)

@@ -135,8 +135,8 @@ def tile_recurrentsig_kernel(
             return None
 
         load_activations(0, load_scale_slot)
-        load_weight_words(0)
         load_activations(1, nothing)
+        load_weight_words(0)
         load_weight_words(1)
         load_activations(2, nothing)
 
@@ -179,29 +179,36 @@ def tile_recurrentsig_kernel(
                 in_=grouped[:, 0 : count * K_PASS],
             )
 
-        def tensor_part(i, part):
-            bt, half = cells[i]
-            cols = slice(half * HALF, (half + 1) * HALF)
-            if part == 0:
-                accs[i] = psum_acc.tile([P, HALF], F32, tag="acc", name="acc%d" % i)
-            if part == 0 and half == 0:
+        def prepare(bt, run):
+            if run == 0:
                 a_words[bt] = quant.tile([P, GROUPS, P], U32, align_bytes=64, tag="a_words", name="a_words%d" % bt)
                 a_scales[bt] = quant.tile([P, GROUPS, P], U8, align_bytes=64, tag="a_scales", name="a_scales%d" % bt)
-            if part < RUNS and half == 0:
-                end = min((part + 1) * RUN, GROUPS)
-                for first in range(part * RUN, end, ROUND):
-                    transpose_and_quantise(bt, first, min(ROUND, end - first))
-            if part > 0:
-                for g in range((part - 1) * RUN, min(part * RUN, GROUPS)):
-                    nc.tensor.matmul_mx(
-                        out=accs[i][:],
-                        lhsT=a_words[bt][:, g, :].bitcast(FP8X4),
-                        lhsT_scale=a_scales[bt][:, g, :],
-                        rhs=w_words[:, g, cols].bitcast(FP8X4),
-                        rhs_scale=w_planes[4 * (g % PLANES_PER_SLOT) : P, g // PLANES_PER_SLOT, cols],
-                        start=(g == 0),
-                        stop=(g == GROUPS - 1),
-                    )
+            end = min((run + 1) * RUN, GROUPS)
+            for first in range(run * RUN, end, ROUND):
+                transpose_and_quantise(bt, first, min(ROUND, end - first))
+
+        def passes(i, run):
+            bt, half = cells[i]
+            cols = slice(half * HALF, (half + 1) * HALF)
+            if run == 0:
+                accs[i] = psum_acc.tile([P, HALF], F32, tag="acc", name="acc%d" % i)
+            for g in range(run * RUN, min((run + 1) * RUN, GROUPS)):
+                nc.tensor.matmul_mx(
+                    out=accs[i][:],
+                    lhsT=a_words[bt][:, g, :].bitcast(FP8X4),
+                    lhsT_scale=a_scales[bt][:, g, :],
+                    rhs=w_words[:, g, cols].bitcast(FP8X4),
+                    rhs_scale=w_planes[4 * (g % PLANES_PER_SLOT) : P, g // PLANES_PER_SLOT, cols],
+                    start=(g == 0),
+                    stop=(g == GROUPS - 1),
+                )
+
+        def tensor_step(i, step):
+            bt, half = cells[i]
+            if half == 0 and step < RUNS:
+                prepare(bt, step)
+            if step > 0:
+                passes(i, step - 1)
 
         plane_sets = [const.tile([P, SIG, HALF], F32, name="planes%d" % s) for s in range(2)]
 
@@ -264,14 +271,18 @@ def tile_recurrentsig_kernel(
         cells = [(bt, half) for pair in range(0, TILES, 2) for half in range(HALVES) for bt in (pair, pair + 1)]
         accs = {}
 
-        for part in range(STEPS):
-            tensor_part(0, part)
+        for bt in range(2):
+            for run in range(RUNS):
+                prepare(bt, run)
+        for run in range(RUNS):
+            for i in range(2):
+                passes(i, run)
         for planes in plane_sets:
             nc.vector.tensor_copy(out=planes[:, 1, :], in_=tl[:, 0:1].to_broadcast([P, HALF]))
         for i in range(-1, len(cells)):
             for step in range(STEPS):
-                if i + 2 < len(cells):
-                    tensor_part(i + 2, step)
+                if 2 <= i + 2 < len(cells):
+                    tensor_step(i + 2, step)
                 if i + 1 < len(cells):
                     plane_step(i + 1, step)
                 if i >= 0:

@@ -29,12 +29,12 @@ SIG_GROUPS = HALF * SIG // K_PASS
 ROUND = 2
 RUN = SIG_GROUPS
 RUNS = -(-GROUPS // RUN)
+ROUNDS = -(-GROUPS // ROUND)
 PLANES_PER_SLOT = 4
 PIECE = 128
 PAIR = 2
-STORE = 2 * PIECE
-LOADED_FIRST = 3
 STEPS = RUNS + 1
+LEAD = 2
 assert HALF // PIECE == STEPS
 
 FLOPS = 2 * BATCH * K_ALL * UNITS
@@ -58,13 +58,13 @@ def tile_recurrentsig_kernel(
     with ExitStack() as ctx:
         ctx.enter_context(tc.manual_schedule())
         const = ctx.enter_context(tc.tile_pool(name="const", bufs=1))
-        sig_pool = ctx.enter_context(tc.tile_pool(name="sig_pool", bufs=LOADED_FIRST * HALVES))
+        sig_pool = ctx.enter_context(tc.tile_pool(name="sig_pool", bufs=TILES * HALVES))
         rest_pool = ctx.enter_context(tc.tile_pool(name="rest_pool", bufs=TILES))
         quant = ctx.enter_context(tc.tile_pool(name="quant", bufs=2))
-        stage = ctx.enter_context(tc.tile_pool(name="stage", bufs=4))
+        stage = ctx.enter_context(tc.tile_pool(name="stage", bufs=ROUNDS))
         small = ctx.enter_context(tc.tile_pool(name="small", bufs=2))
         raws = ctx.enter_context(tc.tile_pool(name="raws", bufs=3))
-        joins = ctx.enter_context(tc.tile_pool(name="joins", bufs=6))
+        joins = ctx.enter_context(tc.tile_pool(name="joins", bufs=8))
         psum_t = ctx.enter_context(tc.psum_pool(name="psum_t", bufs=4))
         psum_acc = ctx.enter_context(tc.psum_pool(name="psum_acc", bufs=4))
 
@@ -135,10 +135,11 @@ def tile_recurrentsig_kernel(
             return None
 
         load_activations(0, load_scale_slot)
-        load_activations(1, nothing)
         load_weight_words(0)
+        load_activations(1, nothing)
         load_weight_words(1)
         load_activations(2, nothing)
+        load_activations(3, nothing)
 
         tl = const.tile([P, 1], F32)
         nc.scalar.activation(out=tl[:], in_=log_tl[:], func=FUNC.Exp)
@@ -162,30 +163,36 @@ def tile_recurrentsig_kernel(
                 source, local = rest_tiles[bt], g - HALVES * SIG_GROUPS
             return source[:, local * K_PASS : (local + 1) * K_PASS].bitcast(F32)
 
-        def transpose_and_quantise(bt, first, count):
-            turned = psum_t.tile([P, ROUND, 2, P], F32, tag="turned")
-            for i in range(count):
-                words = group_words(bt, first + i)
-                for u in range(2):
-                    nc.tensor.transpose(turned[:, i, u, :], words[:, u:WORDS:2], ident[:])
-            grouped = stage.tile([P, ROUND * K_PASS], BF16, align_bytes=64)
-            nc.scalar.copy(
-                out=grouped[:, 0 : count * K_PASS].bitcast(F32).rearrange("p (g b u) -> p g b u", g=count, u=2),
-                in_=turned[:, 0:count].rearrange("p g u b -> p g b u"),
-            )
-            nc.vector.quantize_mx(
-                out=a_words[bt][:, first : first + count, :].rearrange("p g b -> p (g b)").bitcast(FP8X4),
-                scales=a_scales[bt][:, first : first + count, :].rearrange("p g b -> p (g b)"),
-                in_=grouped[:, 0 : count * K_PASS],
-            )
+        grouped_tiles = {}
 
-        def prepare(bt, run):
+        def rounds_of(run):
+            end = min((run + 1) * RUN, GROUPS)
+            return [(first, min(ROUND, end - first)) for first in range(run * RUN, end, ROUND)]
+
+        def turn(bt, run):
+            for first, count in rounds_of(run):
+                turned = psum_t.tile([P, ROUND, 2, P], F32, tag="turned")
+                for i in range(count):
+                    words = group_words(bt, first + i)
+                    for u in range(2):
+                        nc.tensor.transpose(turned[:, i, u, :], words[:, u:WORDS:2], ident[:])
+                grouped = stage.tile([P, ROUND * K_PASS], BF16, align_bytes=64)
+                grouped_tiles[bt, first] = grouped
+                nc.scalar.copy(
+                    out=grouped[:, 0 : count * K_PASS].bitcast(F32).rearrange("p (g b u) -> p g b u", g=count, u=2),
+                    in_=turned[:, 0:count].rearrange("p g u b -> p g b u"),
+                )
+
+        def quantise(bt, run):
             if run == 0:
                 a_words[bt] = quant.tile([P, GROUPS, P], U32, align_bytes=64, tag="a_words", name="a_words%d" % bt)
                 a_scales[bt] = quant.tile([P, GROUPS, P], U8, align_bytes=64, tag="a_scales", name="a_scales%d" % bt)
-            end = min((run + 1) * RUN, GROUPS)
-            for first in range(run * RUN, end, ROUND):
-                transpose_and_quantise(bt, first, min(ROUND, end - first))
+            for first, count in rounds_of(run):
+                nc.vector.quantize_mx(
+                    out=a_words[bt][:, first : first + count, :].rearrange("p g b -> p (g b)").bitcast(FP8X4),
+                    scales=a_scales[bt][:, first : first + count, :].rearrange("p g b -> p (g b)"),
+                    in_=grouped_tiles[bt, first][:, 0 : count * K_PASS],
+                )
 
         def passes(i, run):
             bt, half = cells[i]
@@ -206,7 +213,7 @@ def tile_recurrentsig_kernel(
         def tensor_step(i, step):
             bt, half = cells[i]
             if half == 0 and step < RUNS:
-                prepare(bt, step)
+                quantise(bt, step)
             if step > 0:
                 passes(i, step - 1)
 
@@ -246,48 +253,39 @@ def tile_recurrentsig_kernel(
                     out=planes[:, 2:5:2, :], in0=c[:], in1=planes[:, 0:1, :].to_broadcast([P, 2, HALF]), op=ALU.mult
                 )
 
-        joined_tiles = {}
-
         def join_piece(i, piece):
             bt, half = cells[i]
             n0 = piece * PIECE
-            if n0 % STORE == 0:
-                joined_tiles[i] = joins.tile([P, STORE * SIG], F32, tag="joined", name="joined%d_%d" % (i, piece))
-            joined = joined_tiles[i]
+            joined = joins.tile([P, PIECE * SIG], F32)
             nc.vector.tensor_tensor(
-                out=joined[:, (n0 % STORE) * SIG : (n0 % STORE + PIECE) * SIG].rearrange(
-                    "p (m r j) -> p m j r", r=PAIR, j=SIG
-                ),
+                out=joined[:].rearrange("p (m r j) -> p m j r", r=PAIR, j=SIG),
                 in0=plane_sets[i % 2][:, :, n0 : n0 + PIECE].rearrange("p j (m r) -> p m j r", r=PAIR),
                 in1=sig_tiles[bt, half][:, n0 * SIG : (n0 + PIECE) * SIG].rearrange(
                     "p (m r j) -> p m j r", r=PAIR, j=SIG
                 ),
                 op=ALU.add,
             )
-            if (n0 + PIECE) % STORE == 0:
-                first_col = (half * HALF + n0 + PIECE - STORE) * SIG
-                nc.sync.dma_start(out=out[bt * P : (bt + 1) * P, first_col : first_col + STORE * SIG], in_=joined[:])
+            first_col = (half * HALF + n0) * SIG
+            nc.sync.dma_start(out=out[bt * P : (bt + 1) * P, first_col : first_col + PIECE * SIG], in_=joined[:])
 
         cells = [(bt, half) for pair in range(0, TILES, 2) for half in range(HALVES) for bt in (pair, pair + 1)]
         accs = {}
 
-        for bt in range(2):
-            for run in range(RUNS):
-                prepare(bt, run)
         for run in range(RUNS):
-            for i in range(2):
-                passes(i, run)
+            turn(0, run)
+        for step in range(STEPS):
+            tensor_step(0, step)
         for planes in plane_sets:
             nc.vector.tensor_copy(out=planes[:, 1, :], in_=tl[:, 0:1].to_broadcast([P, HALF]))
-        for i in range(-1, len(cells)):
+        for i in range(-2, len(cells)):
             for step in range(STEPS):
-                if 2 <= i + 2 < len(cells):
+                ahead = STEPS * i + step + LEAD
+                k, run = ahead // STEPS + 2, ahead % STEPS
+                if 1 <= k < len(cells) and cells[k][1] == 0 and run < RUNS:
+                    turn(cells[k][0], run)
+                if 1 <= i + 2 < len(cells):
                     tensor_step(i + 2, step)
-                if i + 1 < len(cells):
+                if 0 <= i + 1 < len(cells):
                     plane_step(i + 1, step)
                 if i >= 0:
                     join_piece(i, step)
-            if i >= 0:
-                bt, half = cells[i]
-                if half == 0 and bt % 2 == 1 and LOADED_FIRST <= bt + 2 < TILES:
-                    load_activations(bt + 2, nothing)

@@ -31,11 +31,10 @@ RUN = SIG_GROUPS
 RUNS = -(-GROUPS // RUN)
 ROUNDS = -(-GROUPS // ROUND)
 PLANES_PER_SLOT = 4
-PIECE = 128
+QUARTER = UNITS // 4
+STEPS = 4
+STORE = 128
 PAIR = 2
-STEPS = RUNS + 1
-LEAD = 2
-assert HALF // PIECE == STEPS
 
 FLOPS = 2 * BATCH * K_ALL * UNITS
 
@@ -58,48 +57,49 @@ def tile_recurrentsig_kernel(
     with ExitStack() as ctx:
         ctx.enter_context(tc.manual_schedule())
         const = ctx.enter_context(tc.tile_pool(name="const", bufs=1))
-        sig_pool = ctx.enter_context(tc.tile_pool(name="sig_pool", bufs=TILES * HALVES))
+        sig_pool = ctx.enter_context(tc.tile_pool(name="sig_pool", bufs=TILES * HALVES - 1))
         rest_pool = ctx.enter_context(tc.tile_pool(name="rest_pool", bufs=TILES))
-        quant = ctx.enter_context(tc.tile_pool(name="quant", bufs=2))
-        stage = ctx.enter_context(tc.tile_pool(name="stage", bufs=ROUNDS))
+        quant = ctx.enter_context(tc.tile_pool(name="quant", bufs=TILES - 1))
+        stage = ctx.enter_context(tc.tile_pool(name="stage", bufs=6))
         small = ctx.enter_context(tc.tile_pool(name="small", bufs=2))
-        raws = ctx.enter_context(tc.tile_pool(name="raws", bufs=3))
-        joins = ctx.enter_context(tc.tile_pool(name="joins", bufs=8))
+        raws = ctx.enter_context(tc.tile_pool(name="raws", bufs=5))
+        joins = ctx.enter_context(tc.tile_pool(name="joins", bufs=10))
         psum_t = ctx.enter_context(tc.psum_pool(name="psum_t", bufs=4))
         psum_acc = ctx.enter_context(tc.psum_pool(name="psum_acc", bufs=4))
 
         w_words = const.tile([P, GROUPS, UNITS], U32, align_bytes=64)
         w_planes = const.tile([P, PLANES_PER_SLOT, UNITS], U8, align_bytes=64)
-        nc.vector.memset(w_planes[:].bitcast(I32), 0)
-
-        ident = const.tile([P, P], F32)
-        make_identity(nc, ident[:])
+        for slot in range(PLANES_PER_SLOT):
+            nc.vector.memset(w_planes[:, slot, :].bitcast(I32), 0)
 
         bias_rows = const.tile([P, UNITS], BF16)
         nc.vector.memset(bias_rows[:], 0.0)
         ones = const.tile([P, P], BF16)
         nc.vector.memset(ones[:], 1.0)
-        nc.scalar.dma_start(out=bias_rows[0:1, :], in_=W_b.unsqueeze(0))
-        nc.scalar.dma_start(out=bias_rows[1:2, :], in_=U_b.unsqueeze(0))
+        ident = const.tile([P, P], F32)
         log_tl = const.tile([P, 1], BF16)
-        nc.scalar.dma_start(out=log_tl[:], in_=log_timelapse.partition_broadcast(P))
 
         sig_tiles = {}
         rest_tiles = {}
 
-        def load_activations(bt, behind_each_load):
+        def load_sigs(queue, bt, half):
+            sigs = sig_pool.tile([P, HALF * SIG], BF16, tag="sigs", name="sigs%d_%d" % (bt, half))
+            sig_tiles[bt, half] = sigs
+            queue.dma_start(
+                out=sigs[:], in_=prev_sigs[bt * P : (bt + 1) * P, half * HALF * SIG : (half + 1) * HALF * SIG]
+            )
+
+        def load_rest(queue, bt):
             rows = slice(bt * P, (bt + 1) * P)
-            for half in range(HALVES):
-                sigs = sig_pool.tile([P, HALF * SIG], BF16, tag="sigs", name="sigs%d_%d" % (bt, half))
-                sig_tiles[bt, half] = sigs
-                nc.sync.dma_start(out=sigs[:], in_=prev_sigs[rows, half * HALF * SIG : (half + 1) * HALF * SIG])
-                behind_each_load(half)
             rest = rest_pool.tile([P, UNITS + INPUTS], BF16, tag="rest", name="rest%d" % bt)
             rest_tiles[bt] = rest
-            nc.sync.dma_start(out=rest[:, 0:UNITS], in_=prev_states[rows, :])
-            behind_each_load(HALVES)
-            nc.sync.dma_start(out=rest[:, UNITS : UNITS + INPUTS], in_=x[rows, :])
-            behind_each_load(HALVES + 1)
+            queue.dma_start(out=rest[:, 0:UNITS], in_=prev_states[rows, :])
+            queue.dma_start(out=rest[:, UNITS : UNITS + INPUTS], in_=x[rows, :])
+
+        def load_activations(bt):
+            for half in range(HALVES):
+                load_sigs(nc.sync, bt, half)
+            load_rest(nc.sync, bt)
 
         def load_scale_slot(slot):
             first = slot * PLANES_PER_SLOT
@@ -118,8 +118,8 @@ def tile_recurrentsig_kernel(
                         in_=W_w_scales[0, rows, :].bitcast(I32),
                     )
 
-        def load_weight_words(half):
-            cols = slice(half * HALF, (half + 1) * HALF)
+        def load_weight_words(unit0, units):
+            cols = slice(unit0, unit0 + units)
             for first in range(0, U_GROUPS, RUN):
                 last = min(first + RUN, U_GROUPS)
                 nc.sync.dma_start(
@@ -131,27 +131,21 @@ def tile_recurrentsig_kernel(
                 in_=W_w_words[0, :, cols, :].rearrange("p n t -> p (n t)").bitcast(I32),
             )
 
-        def nothing(i):
-            return None
+        load_sigs(nc.gpsimd, 0, 0)
+        make_identity(nc, ident[:])
+        load_sigs(nc.gpsimd, 0, 1)
+        load_rest(nc.sync, 0)
+        nc.scalar.dma_start(out=bias_rows[0:1, :], in_=W_b.unsqueeze(0))
+        nc.scalar.dma_start(out=bias_rows[1:2, :], in_=U_b.unsqueeze(0))
+        nc.scalar.dma_start(out=log_tl[:], in_=log_timelapse.partition_broadcast(P))
 
-        load_activations(0, load_scale_slot)
-        load_weight_words(0)
-        load_activations(1, nothing)
-        load_weight_words(1)
-        load_activations(2, nothing)
-        load_activations(3, nothing)
-
-        tl = const.tile([P, 1], F32)
-        nc.scalar.activation(out=tl[:], in_=log_tl[:], func=FUNC.Exp)
-        half_tl = const.tile([P, 1], F32)
-        nc.scalar.mul(out=half_tl[:], in_=tl[:], mul=0.5)
-
-        bias = const.tile([P, UNITS], F32)
-        for half in range(HALVES):
-            cols = slice(half * HALF, (half + 1) * HALF)
-            bias_ps = psum_acc.tile([P, HALF], F32, tag="acc")
-            nc.tensor.matmul(out=bias_ps[:], lhsT=ones[:], rhs=bias_rows[:, cols], start=True, stop=True)
-            nc.vector.tensor_copy(out=bias[:, cols], in_=bias_ps[:])
+        for slot in range(PLANES_PER_SLOT):
+            load_scale_slot(slot)
+        load_weight_words(0, QUARTER)
+        load_activations(1)
+        load_weight_words(QUARTER, QUARTER)
+        load_activations(2)
+        load_weight_words(HALF, HALF)
 
         a_words = {}
         a_scales = {}
@@ -195,13 +189,13 @@ def tile_recurrentsig_kernel(
                 )
 
         def passes(i, run):
-            bt, half = cells[i]
-            cols = slice(half * HALF, (half + 1) * HALF)
+            bt, unit0, units = cells[i]
+            cols = slice(unit0, unit0 + units)
             if run == 0:
                 accs[i] = psum_acc.tile([P, HALF], F32, tag="acc", name="acc%d" % i)
             for g in range(run * RUN, min((run + 1) * RUN, GROUPS)):
                 nc.tensor.matmul_mx(
-                    out=accs[i][:],
+                    out=accs[i][:, 0:units],
                     lhsT=a_words[bt][:, g, :].bitcast(FP8X4),
                     lhsT_scale=a_scales[bt][:, g, :],
                     rhs=w_words[:, g, cols].bitcast(FP8X4),
@@ -210,82 +204,136 @@ def tile_recurrentsig_kernel(
                     stop=(g == GROUPS - 1),
                 )
 
-        def tensor_step(i, step):
-            bt, half = cells[i]
-            if half == 0 and step < RUNS:
-                quantise(bt, step)
-            if step > 0:
-                passes(i, step - 1)
-
         plane_sets = [const.tile([P, SIG, HALF], F32, name="planes%d" % s) for s in range(2)]
 
         cell_tiles = {}
 
         def plane_step(i, step):
-            bt, half = cells[i]
+            bt, unit0, units = cells[i]
+            half, u = divmod(unit0, HALF)
             planes = plane_sets[i % 2]
             if step == 0:
-                by_unit = sig_tiles[bt, half][:].rearrange("p (n j) -> p n j", j=SIG)
+                by_unit = sig_tiles[bt, half][:, u * SIG : (u + units) * SIG].rearrange("p (n j) -> p n j", j=SIG)
                 a0 = small.tile([P, HALF], BF16)
-                nc.scalar.copy(out=a0[:], in_=by_unit[:, :, 0])
+                nc.scalar.copy(out=a0[:, 0:units], in_=by_unit[:, :, 0])
                 c = small.tile([P, 2, HALF], F32)
                 nc.scalar.activation(
-                    out=c[:, 1, :], in_=by_unit[:, :, 1], func=FUNC.Identity, bias=half_tl[:, 0:1], scale=1.0
+                    out=c[:, 1, 0:units], in_=by_unit[:, :, 1], func=FUNC.Identity, bias=half_tl[:, 0:1], scale=1.0
                 )
                 raw = raws.tile([P, HALF], F32)
                 cell_tiles[i] = (a0, c, raw)
                 nc.vector.tensor_tensor(
-                    out=raw[:], in0=accs[i][:], in1=bias[:, half * HALF : (half + 1) * HALF], op=ALU.add
+                    out=raw[:, 0:units], in0=accs[i][:, 0:units], in1=bias[:, unit0 : unit0 + units], op=ALU.add
                 )
-                first_col = UNITS * SIG + half * HALF
-                nc.sync.dma_start(out=out[bt * P : (bt + 1) * P, first_col : first_col + HALF], in_=raw[:])
+                first_col = UNITS * SIG + unit0
+                nc.sync.dma_start(
+                    out=out[bt * P : (bt + 1) * P, first_col : first_col + units], in_=raw[:, 0:units]
+                )
             a0, c, raw = cell_tiles[i]
             if step == 1:
-                states = rest_tiles[bt][:, half * HALF : (half + 1) * HALF]
-                nc.vector.tensor_tensor(out=planes[:, 0, :], in0=raw[:], in1=states, op=ALU.subtract)
+                states = rest_tiles[bt][:, unit0 : unit0 + units]
+                nc.vector.tensor_tensor(
+                    out=planes[:, 0, 0:units], in0=raw[:, 0:units], in1=states, op=ALU.subtract
+                )
             if step == 2:
                 nc.vector.scalar_tensor_tensor(
-                    out=c[:, 0, :], in0=planes[:, 0, :], scalar=0.5, in1=a0[:], op0=ALU.mult, op1=ALU.add
+                    out=c[:, 0, 0:units],
+                    in0=planes[:, 0, 0:units],
+                    scalar=0.5,
+                    in1=a0[:, 0:units],
+                    op0=ALU.mult,
+                    op1=ALU.add,
                 )
-                nc.scalar.activation(out=planes[:, 3:6:2, :], in_=c[:], func=FUNC.Copy, scale=tl[:, 0:1])
+                nc.scalar.activation(
+                    out=planes[:, 3:6:2, 0:units], in_=c[:, :, 0:units], func=FUNC.Copy, scale=tl[:, 0:1]
+                )
             if step == 3:
                 nc.vector.tensor_tensor(
-                    out=planes[:, 2:5:2, :], in0=c[:], in1=planes[:, 0:1, :].to_broadcast([P, 2, HALF]), op=ALU.mult
+                    out=planes[:, 2:5:2, 0:units],
+                    in0=c[:, :, 0:units],
+                    in1=planes[:, 0:1, 0:units].to_broadcast([P, 2, units]),
+                    op=ALU.mult,
                 )
 
+        joined_tiles = {}
+
         def join_piece(i, piece):
-            bt, half = cells[i]
-            n0 = piece * PIECE
-            joined = joins.tile([P, PIECE * SIG], F32)
+            bt, unit0, units = cells[i]
+            half, u = divmod(unit0, HALF)
+            count = units // STEPS
+            n0 = piece * count
+            at = n0 % STORE
+            if at == 0:
+                joined_tiles[i] = joins.tile([P, STORE * SIG], F32, tag="joined", name="joined%d_%d" % (i, piece))
+            joined = joined_tiles[i]
             nc.vector.tensor_tensor(
-                out=joined[:].rearrange("p (m r j) -> p m j r", r=PAIR, j=SIG),
-                in0=plane_sets[i % 2][:, :, n0 : n0 + PIECE].rearrange("p j (m r) -> p m j r", r=PAIR),
-                in1=sig_tiles[bt, half][:, n0 * SIG : (n0 + PIECE) * SIG].rearrange(
+                out=joined[:, at * SIG : (at + count) * SIG].rearrange("p (m r j) -> p m j r", r=PAIR, j=SIG),
+                in0=plane_sets[i % 2][:, :, n0 : n0 + count].rearrange("p j (m r) -> p m j r", r=PAIR),
+                in1=sig_tiles[bt, half][:, (u + n0) * SIG : (u + n0 + count) * SIG].rearrange(
                     "p (m r j) -> p m j r", r=PAIR, j=SIG
                 ),
                 op=ALU.add,
             )
-            first_col = (half * HALF + n0) * SIG
-            nc.sync.dma_start(out=out[bt * P : (bt + 1) * P, first_col : first_col + PIECE * SIG], in_=joined[:])
+            if at + count == STORE:
+                first_col = (unit0 + n0 + count - STORE) * SIG
+                nc.sync.dma_start(out=out[bt * P : (bt + 1) * P, first_col : first_col + STORE * SIG], in_=joined[:])
 
-        cells = [(bt, half) for pair in range(0, TILES, 2) for half in range(HALVES) for bt in (pair, pair + 1)]
+        cells = [(bt, unit0, QUARTER) for unit0 in (0, QUARTER) for bt in (0, 1)]
+        cells += [(2, 0, HALF), (0, HALF, HALF), (1, HALF, HALF), (2, HALF, HALF), (3, 0, HALF), (3, HALF, HALF)]
         accs = {}
 
         for run in range(RUNS):
             turn(0, run)
-        for step in range(STEPS):
-            tensor_step(0, step)
+            quantise(0, run)
+        tl = const.tile([P, 1], F32)
+        nc.scalar.activation(out=tl[:], in_=log_tl[:], func=FUNC.Exp)
+        half_tl = const.tile([P, 1], F32)
+        nc.scalar.mul(out=half_tl[:], in_=tl[:], mul=0.5)
+        bias = const.tile([P, UNITS], F32)
+        for half in range(HALVES):
+            cols = slice(half * HALF, (half + 1) * HALF)
+            bias_ps = psum_acc.tile([P, HALF], F32, tag="acc")
+            nc.tensor.matmul(out=bias_ps[:], lhsT=ones[:], rhs=bias_rows[:, cols], start=True, stop=True)
+            nc.vector.tensor_copy(out=bias[:, cols], in_=bias_ps[:])
         for planes in plane_sets:
             nc.vector.tensor_copy(out=planes[:, 1, :], in_=tl[:, 0:1].to_broadcast([P, HALF]))
-        for i in range(-2, len(cells)):
+
+        for run in range(RUNS):
+            passes(0, run)
+        for step in range(STEPS):
+            plane_step(0, step)
+        for step in range(STEPS):
+            join_piece(0, step)
+        for run in range(RUNS):
+            turn(1, run)
+            quantise(1, run)
+        for run in range(RUNS):
+            passes(1, run)
+        for step in range(STEPS):
+            plane_step(1, step)
+        for run in range(RUNS):
+            passes(2, run)
+
+        turns = {(2, 0): [(2, 0)], (2, 1): [(2, 1)], (2, 2): [(2, 2)], (5, 2): [(3, 0)], (5, 3): [(3, 1)], (6, 0): [(3, 2)]}
+        quants = {(2, 2): (2, 0), (2, 3): (2, 1), (3, 0): (2, 2), (6, 0): (3, 0), (6, 1): (3, 1), (6, 2): (3, 2)}
+        for i in range(1, len(cells)):
             for step in range(STEPS):
-                ahead = STEPS * i + step + LEAD
-                k, run = ahead // STEPS + 2, ahead % STEPS
-                if 1 <= k < len(cells) and cells[k][1] == 0 and run < RUNS:
-                    turn(cells[k][0], run)
-                if 1 <= i + 2 < len(cells):
-                    tensor_step(i + 2, step)
-                if 0 <= i + 1 < len(cells):
-                    plane_step(i + 1, step)
-                if i >= 0:
+                for bt, run in turns.get((i, step), []):
+                    turn(bt, run)
+                if (i, step) in quants:
+                    quantise(*quants[i, step])
+                if i == 2 and step == 3:
+                    passes(4, 0)
+                elif i == 3 and step == 0:
+                    passes(4, 1)
+                    passes(4, 2)
+                if i != 2 and step > 0 and i + 2 < len(cells):
+                    passes(i + 2, step - 1)
+                if i == 3:
                     join_piece(i, step)
+                if i + 1 < len(cells):
+                    plane_step(i + 1, step)
+                if i != 3:
+                    join_piece(i, step)
+            if i == 2:
+                load_activations(3)

@@ -69,11 +69,11 @@ def tile_recurrentsig_kernel(
 
         w_words = const.tile([P, GROUPS, UNITS], U32, align_bytes=64)
         w_planes = const.tile([P, PLANES_PER_SLOT, UNITS], U8, align_bytes=64)
-        for slot in range(PLANES_PER_SLOT):
-            nc.vector.memset(w_planes[:, slot, :].bitcast(I32), 0)
-
+        nc.vector.memset(w_planes[:, 0, :].bitcast(I32), 0)
         bias_rows = const.tile([P, UNITS], BF16)
-        nc.vector.memset(bias_rows[:], 0.0)
+        nc.vector.memset(bias_rows[:].bitcast(I32), 0)
+        for slot in range(1, PLANES_PER_SLOT):
+            nc.vector.memset(w_planes[:, slot, :].bitcast(I32), 0)
         ones = const.tile([P, P], BF16)
         nc.vector.memset(ones[:], 1.0)
         ident = const.tile([P, P], F32)
@@ -82,24 +82,24 @@ def tile_recurrentsig_kernel(
         sig_tiles = {}
         rest_tiles = {}
 
-        def load_sigs(queue, bt, half):
+        def load_sigs(bt, half):
             sigs = sig_pool.tile([P, HALF * SIG], BF16, tag="sigs", name="sigs%d_%d" % (bt, half))
             sig_tiles[bt, half] = sigs
-            queue.dma_start(
+            nc.sync.dma_start(
                 out=sigs[:], in_=prev_sigs[bt * P : (bt + 1) * P, half * HALF * SIG : (half + 1) * HALF * SIG]
             )
 
-        def load_rest(queue, bt):
+        def load_rest(bt):
             rows = slice(bt * P, (bt + 1) * P)
             rest = rest_pool.tile([P, UNITS + INPUTS], BF16, tag="rest", name="rest%d" % bt)
             rest_tiles[bt] = rest
-            queue.dma_start(out=rest[:, 0:UNITS], in_=prev_states[rows, :])
-            queue.dma_start(out=rest[:, UNITS : UNITS + INPUTS], in_=x[rows, :])
+            nc.sync.dma_start(out=rest[:, 0:UNITS], in_=prev_states[rows, :])
+            nc.sync.dma_start(out=rest[:, UNITS : UNITS + INPUTS], in_=x[rows, :])
 
         def load_activations(bt):
             for half in range(HALVES):
-                load_sigs(nc.sync, bt, half)
-            load_rest(nc.sync, bt)
+                load_sigs(bt, half)
+            load_rest(bt)
 
         def load_scale_slot(slot):
             first = slot * PLANES_PER_SLOT
@@ -118,7 +118,7 @@ def tile_recurrentsig_kernel(
                         in_=W_w_scales[0, rows, :].bitcast(I32),
                     )
 
-        def load_weight_words(unit0, units):
+        def load_weight_words(unit0, units, behind_each_load):
             cols = slice(unit0, unit0 + units)
             for first in range(0, U_GROUPS, RUN):
                 last = min(first + RUN, U_GROUPS)
@@ -126,26 +126,33 @@ def tile_recurrentsig_kernel(
                     out=w_words[:, first:last, cols].bitcast(I32),
                     in_=U_w_words[first:last, :, cols, :].rearrange("g p n t -> p g (n t)").bitcast(I32),
                 )
+                behind_each_load(first // RUN)
             nc.sync.dma_start(
                 out=w_words[:, U_GROUPS, cols].bitcast(I32),
                 in_=W_w_words[0, :, cols, :].rearrange("p n t -> p (n t)").bitcast(I32),
             )
 
-        load_sigs(nc.gpsimd, 0, 0)
-        make_identity(nc, ident[:])
-        load_sigs(nc.gpsimd, 0, 1)
-        load_rest(nc.sync, 0)
-        nc.scalar.dma_start(out=bias_rows[0:1, :], in_=W_b.unsqueeze(0))
-        nc.scalar.dma_start(out=bias_rows[1:2, :], in_=U_b.unsqueeze(0))
-        nc.scalar.dma_start(out=log_tl[:], in_=log_timelapse.partition_broadcast(P))
+        def nothing(run):
+            return None
 
-        for slot in range(PLANES_PER_SLOT):
-            load_scale_slot(slot)
-        load_weight_words(0, QUARTER)
+        def third_slot(run):
+            if run == 1:
+                load_scale_slot(2)
+
+        make_identity(nc, ident[:])
+        nc.gpsimd.dma_start(out=log_tl[:], in_=log_timelapse.partition_broadcast(P))
+        nc.gpsimd.dma_start(out=bias_rows[0:1, :], in_=W_b.unsqueeze(0))
+        nc.gpsimd.dma_start(out=bias_rows[1:2, :], in_=U_b.unsqueeze(0))
+
+        load_scale_slot(0)
+        load_activations(0)
+        load_scale_slot(1)
+        load_weight_words(0, QUARTER, third_slot)
+        load_scale_slot(3)
         load_activations(1)
-        load_weight_words(QUARTER, QUARTER)
+        load_weight_words(QUARTER, QUARTER, nothing)
         load_activations(2)
-        load_weight_words(HALF, HALF)
+        load_weight_words(HALF, HALF, nothing)
 
         a_words = {}
         a_scales = {}

@@ -101,10 +101,10 @@ def tile_recurrentsig_kernel(
                 load_sigs(bt, half)
             load_rest(bt)
 
-        def load_scale_slot(slot):
+        def load_scale_slot(slot, quadrants=(0, 1, 2, 3)):
             first = slot * PLANES_PER_SLOT
             last = min(first + PLANES_PER_SLOT, U_GROUPS)
-            for quadrant in range(4):
+            for quadrant in quadrants:
                 top = 32 * quadrant
                 rows = slice(4 * quadrant, 4 * quadrant + 4)
                 nc.sync.dma_start(
@@ -118,7 +118,7 @@ def tile_recurrentsig_kernel(
                         in_=W_w_scales[0, rows, :].bitcast(I32),
                     )
 
-        def load_weight_words(unit0, units, behind_each_load):
+        def load_weight_words(unit0, units, behind_each_load=lambda run: None):
             cols = slice(unit0, unit0 + units)
             for first in range(0, U_GROUPS, RUN):
                 last = min(first + RUN, U_GROUPS)
@@ -132,13 +132,6 @@ def tile_recurrentsig_kernel(
                 in_=W_w_words[0, :, cols, :].rearrange("p n t -> p (n t)").bitcast(I32),
             )
 
-        def nothing(run):
-            return None
-
-        def third_slot(run):
-            if run == 1:
-                load_scale_slot(2)
-
         make_identity(nc, ident[:])
         nc.gpsimd.dma_start(out=log_tl[:], in_=log_timelapse.partition_broadcast(P))
         nc.gpsimd.dma_start(out=bias_rows[0:1, :], in_=W_b.unsqueeze(0))
@@ -147,12 +140,15 @@ def tile_recurrentsig_kernel(
         load_scale_slot(0)
         load_activations(0)
         load_scale_slot(1)
-        load_weight_words(0, QUARTER, third_slot)
-        load_scale_slot(3)
-        load_activations(1)
-        load_weight_words(QUARTER, QUARTER, nothing)
+        load_sigs(1, 0)
+        load_scale_slot(2)
+        load_sigs(1, 1)
+        load_scale_slot(3, (0, 1))
+        load_rest(1)
+        load_weight_words(0, QUARTER, lambda run: load_scale_slot(3, (2, 3)) if run == 1 else None)
+        load_weight_words(QUARTER, QUARTER)
         load_activations(2)
-        load_weight_words(HALF, HALF, nothing)
+        load_weight_words(HALF, HALF)
 
         a_words = {}
         a_scales = {}
@@ -289,9 +285,10 @@ def tile_recurrentsig_kernel(
         cells += [(2, 0, HALF), (0, HALF, HALF), (1, HALF, HALF), (2, HALF, HALF), (3, 0, HALF), (3, HALF, HALF)]
         accs = {}
 
-        for run in range(RUNS):
-            turn(0, run)
-            quantise(0, run)
+        for bt in (0, 1):
+            for run in range(RUNS):
+                turn(bt, run)
+                quantise(bt, run)
         tl = const.tile([P, 1], F32)
         nc.scalar.activation(out=tl[:], in_=log_tl[:], func=FUNC.Exp)
         half_tl = const.tile([P, 1], F32)
@@ -305,34 +302,23 @@ def tile_recurrentsig_kernel(
         for planes in plane_sets:
             nc.vector.tensor_copy(out=planes[:, 1, :], in_=tl[:, 0:1].to_broadcast([P, HALF]))
 
-        for run in range(RUNS):
-            passes(0, run)
+        for i in (0, 1):
+            for run in range(RUNS):
+                passes(i, run)
         for step in range(STEPS):
             plane_step(0, step)
-        for step in range(STEPS):
-            join_piece(0, step)
-        for run in range(RUNS):
-            turn(1, run)
-            quantise(1, run)
-        for run in range(RUNS):
-            passes(1, run)
-        for step in range(STEPS):
-            plane_step(1, step)
-        for run in range(RUNS):
-            passes(2, run)
 
-        turns = {(2, 0): [(2, 0)], (2, 1): [(2, 1)], (2, 2): [(2, 2)], (5, 2): [(3, 0)], (5, 3): [(3, 1)], (6, 0): [(3, 2)]}
-        quants = {(2, 2): (2, 0), (2, 3): (2, 1), (3, 0): (2, 2), (6, 0): (3, 0), (6, 1): (3, 1), (6, 2): (3, 2)}
-        for i in range(1, len(cells)):
+        turns = {(1, 3): [(2, 0)], (2, 0): [(2, 1)], (2, 1): [(2, 2)], (5, 2): [(3, 0)], (5, 3): [(3, 1)], (6, 0): [(3, 2)]}
+        quants = {(2, 1): (2, 0), (2, 2): (2, 1), (2, 3): (2, 2), (6, 0): (3, 0), (6, 1): (3, 1), (6, 2): (3, 2)}
+        for i in range(len(cells)):
             for step in range(STEPS):
                 for bt, run in turns.get((i, step), []):
                     turn(bt, run)
                 if (i, step) in quants:
                     quantise(*quants[i, step])
-                if i == 2 and step == 3:
-                    passes(4, 0)
+                if i == 2 and step > 1:
+                    passes(4, step - 2)
                 elif i == 3 and step == 0:
-                    passes(4, 1)
                     passes(4, 2)
                 if i != 2 and step > 0 and i + 2 < len(cells):
                     passes(i + 2, step - 1)

@@ -62,15 +62,17 @@ def tile_recurrentsig_kernel(
         quant = ctx.enter_context(tc.tile_pool(name="quant", bufs=TILES - 1))
         stage = ctx.enter_context(tc.tile_pool(name="stage", bufs=6))
         small = ctx.enter_context(tc.tile_pool(name="small", bufs=2))
+        turned_sums = ctx.enter_context(tc.tile_pool(name="turned_sums", bufs=2))
         raws = ctx.enter_context(tc.tile_pool(name="raws", bufs=5))
-        joins = ctx.enter_context(tc.tile_pool(name="joins", bufs=10))
+        joins = ctx.enter_context(tc.tile_pool(name="joins", bufs=9))
         psum_t = ctx.enter_context(tc.psum_pool(name="psum_t", bufs=4))
-        psum_acc = ctx.enter_context(tc.psum_pool(name="psum_acc", bufs=4))
+        psum_acc = ctx.enter_context(tc.psum_pool(name="psum_acc", bufs=3))
+        psum_back = ctx.enter_context(tc.psum_pool(name="psum_back", bufs=1))
 
         w_words = const.tile([P, GROUPS, UNITS], U32, align_bytes=64)
         w_planes = const.tile([P, PLANES_PER_SLOT, UNITS], U8, align_bytes=64)
         nc.vector.memset(w_planes[:, 0, :].bitcast(I32), 0)
-        bias_rows = const.tile([P, UNITS], BF16)
+        bias_rows = stage.tile([P, UNITS], BF16, align_bytes=64, tag="stage")
         nc.vector.memset(bias_rows[:].bitcast(I32), 0)
         for slot in range(1, PLANES_PER_SLOT):
             nc.vector.memset(w_planes[:, slot, :].bitcast(I32), 0)
@@ -137,8 +139,10 @@ def tile_recurrentsig_kernel(
         nc.gpsimd.dma_start(out=bias_rows[0:1, :], in_=W_b.unsqueeze(0))
         nc.gpsimd.dma_start(out=bias_rows[1:2, :], in_=U_b.unsqueeze(0))
 
+        load_sigs(0, 0)
         load_scale_slot(0)
-        load_activations(0)
+        load_sigs(0, 1)
+        load_rest(0)
         load_scale_slot(1)
         load_sigs(1, 0)
         load_scale_slot(2)
@@ -148,7 +152,6 @@ def tile_recurrentsig_kernel(
         load_weight_words(0, QUARTER, lambda run: load_scale_slot(3, (2, 3)) if run == 1 else None)
         load_weight_words(QUARTER, QUARTER)
         load_activations(2)
-        load_weight_words(HALF, HALF)
 
         a_words = {}
         a_scales = {}
@@ -173,7 +176,7 @@ def tile_recurrentsig_kernel(
                     words = group_words(bt, first + i)
                     for u in range(2):
                         nc.tensor.transpose(turned[:, i, u, :], words[:, u:WORDS:2], ident[:])
-                grouped = stage.tile([P, ROUND * K_PASS], BF16, align_bytes=64)
+                grouped = stage.tile([P, ROUND * K_PASS], BF16, align_bytes=64, tag="stage")
                 grouped_tiles[bt, first] = grouped
                 nc.scalar.copy(
                     out=grouped[:, 0 : count * K_PASS].bitcast(F32).rearrange("p (g b u) -> p g b u", g=count, u=2),
@@ -191,70 +194,120 @@ def tile_recurrentsig_kernel(
                     in_=grouped_tiles[bt, first][:, 0 : count * K_PASS],
                 )
 
+        def one_pass(g, out, stationary, moving):
+            nc.tensor.matmul_mx(
+                out=out,
+                lhsT=stationary[0],
+                lhsT_scale=stationary[1],
+                rhs=moving[0],
+                rhs_scale=moving[1],
+                start=(g == 0),
+                stop=(g == GROUPS - 1),
+            )
+
+        def weights_of(g, cols):
+            planes = w_planes[4 * (g % PLANES_PER_SLOT) : P, g // PLANES_PER_SLOT, cols]
+            return w_words[:, g, cols].bitcast(FP8X4), planes
+
+        def codes_of(bt, g):
+            return a_words[bt][:, g, :].bitcast(FP8X4), a_scales[bt][:, g, :]
+
         def passes(i, run):
             bt, unit0, units = cells[i]
             cols = slice(unit0, unit0 + units)
             if run == 0:
                 accs[i] = psum_acc.tile([P, HALF], F32, tag="acc", name="acc%d" % i)
             for g in range(run * RUN, min((run + 1) * RUN, GROUPS)):
-                nc.tensor.matmul_mx(
-                    out=accs[i][:, 0:units],
-                    lhsT=a_words[bt][:, g, :].bitcast(FP8X4),
-                    lhsT_scale=a_scales[bt][:, g, :],
-                    rhs=w_words[:, g, cols].bitcast(FP8X4),
-                    rhs_scale=w_planes[4 * (g % PLANES_PER_SLOT) : P, g // PLANES_PER_SLOT, cols],
-                    start=(g == 0),
-                    stop=(g == GROUPS - 1),
+                one_pass(g, accs[i][:, 0:units], codes_of(bt, g), weights_of(g, cols))
+
+        def turned_passes(i, chunk):
+            bt, unit0, units = cells[i]
+            cols = slice(unit0 + chunk * P, unit0 + (chunk + 1) * P)
+            if chunk == 0:
+                accs[i] = psum_acc.tile([P, HALF], F32, tag="acc", name="acc%d" % i)
+            for g in range(GROUPS):
+                out_cols = accs[i][:, chunk * P : (chunk + 1) * P]
+                one_pass(g, out_cols, weights_of(g, cols), codes_of(bt, g))
+
+        def add_bias(i):
+            bt, unit0, units = cells[i]
+            with_bias[i] = turned_sums.tile([P, HALF], F32, tag="with_bias", name="with_bias%d" % i)
+            for chunk in range(HALF // P):
+                cols = slice(chunk * P, (chunk + 1) * P)
+                at = unit0 // P + chunk
+                nc.scalar.activation(
+                    out=with_bias[i][:, cols],
+                    in_=accs[i][:, cols],
+                    func=FUNC.Identity,
+                    bias=bias_cols[:, at : at + 1],
+                    scale=1.0,
                 )
+
+        def turn_back(i):
+            accs[i] = psum_back.tile([P, HALF], F32, tag="back", name="back%d" % i)
+            for chunk in range(HALF // P):
+                cols = slice(chunk * P, (chunk + 1) * P)
+                nc.tensor.transpose(accs[i][:, cols], with_bias[i][:, cols], ident[:])
+
+        with_bias = {}
 
         plane_sets = [const.tile([P, SIG, HALF], F32, name="planes%d" % s) for s in range(2)]
 
         cell_tiles = {}
 
-        def plane_step(i, step):
+        def is_turned(i):
+            return i > 5
+
+        def store_raw(i, raw, unit0, units):
+            bt = cells[i][0]
+            first_col = UNITS * SIG + unit0
+            nc.sync.dma_start(out=out[bt * P : (bt + 1) * P, first_col : first_col + units], in_=raw)
+
+        def plane_step(i, step, lo=0, hi=None):
             bt, unit0, units = cells[i]
+            units = (hi or units) - lo
+            unit0 += lo
             half, u = divmod(unit0, HALF)
-            planes = plane_sets[i % 2]
-            if step == 0:
-                by_unit = sig_tiles[bt, half][:, u * SIG : (u + units) * SIG].rearrange("p (n j) -> p n j", j=SIG)
+            planes = plane_sets[i % 2][:, :, lo : lo + units]
+            if step == 0 and lo == 0:
                 a0 = small.tile([P, HALF], BF16)
-                nc.scalar.copy(out=a0[:, 0:units], in_=by_unit[:, :, 0])
                 c = small.tile([P, 2, HALF], F32)
-                nc.scalar.activation(
-                    out=c[:, 1, 0:units], in_=by_unit[:, :, 1], func=FUNC.Identity, bias=half_tl[:, 0:1], scale=1.0
-                )
                 raw = raws.tile([P, HALF], F32)
                 cell_tiles[i] = (a0, c, raw)
-                nc.vector.tensor_tensor(
-                    out=raw[:, 0:units], in0=accs[i][:, 0:units], in1=bias[:, unit0 : unit0 + units], op=ALU.add
+            a0, c, raw = (
+                cell_tiles[i][0][:, lo : lo + units],
+                cell_tiles[i][1][:, :, lo : lo + units],
+                cell_tiles[i][2][:, lo : lo + units],
+            )
+            if step == 0:
+                by_unit = sig_tiles[bt, half][:, u * SIG : (u + units) * SIG].rearrange("p (n j) -> p n j", j=SIG)
+                nc.scalar.copy(out=a0, in_=by_unit[:, :, 0])
+                nc.scalar.activation(
+                    out=c[:, 1, :], in_=by_unit[:, :, 1], func=FUNC.Identity, bias=half_tl[:, 0:1], scale=1.0
                 )
-                first_col = UNITS * SIG + unit0
-                nc.sync.dma_start(
-                    out=out[bt * P : (bt + 1) * P, first_col : first_col + units], in_=raw[:, 0:units]
-                )
-            a0, c, raw = cell_tiles[i]
+                if not is_turned(i):
+                    nc.vector.tensor_tensor(
+                        out=raw, in0=accs[i][:, lo : lo + units], in1=bias[:, unit0 : unit0 + units], op=ALU.add
+                    )
+                    if lo + units == cells[i][2]:
+                        store_raw(i, cell_tiles[i][2][:, 0 : cells[i][2]], cells[i][1], cells[i][2])
             if step == 1:
                 states = rest_tiles[bt][:, unit0 : unit0 + units]
-                nc.vector.tensor_tensor(
-                    out=planes[:, 0, 0:units], in0=raw[:, 0:units], in1=states, op=ALU.subtract
-                )
+                exact = accs[i][:, 0:units] if is_turned(i) else raw
+                nc.vector.tensor_tensor(out=planes[:, 0, :], in0=exact, in1=states, op=ALU.subtract)
+                if is_turned(i):
+                    nc.scalar.copy(out=raw, in_=accs[i][:, 0:units])
+                    store_raw(i, raw, unit0, units)
             if step == 2:
                 nc.vector.scalar_tensor_tensor(
-                    out=c[:, 0, 0:units],
-                    in0=planes[:, 0, 0:units],
-                    scalar=0.5,
-                    in1=a0[:, 0:units],
-                    op0=ALU.mult,
-                    op1=ALU.add,
+                    out=c[:, 0, :], in0=planes[:, 0, :], scalar=0.5, in1=a0, op0=ALU.mult, op1=ALU.add
                 )
-                nc.scalar.activation(
-                    out=planes[:, 3:6:2, 0:units], in_=c[:, :, 0:units], func=FUNC.Copy, scale=tl[:, 0:1]
-                )
+                nc.scalar.activation(out=planes[:, 3:6:2, :], in_=c, func=FUNC.Copy, scale=tl[:, 0:1])
             if step == 3:
                 nc.vector.tensor_tensor(
-                    out=planes[:, 2:5:2, 0:units],
-                    in0=c[:, :, 0:units],
-                    in1=planes[:, 0:1, 0:units].to_broadcast([P, 2, units]),
+                    out=planes[:, 2:5:2, :],
+                    in0=c,
+                    in1=planes[:, 0:1, :].to_broadcast([P, 2, units]),
                     op=ALU.mult,
                 )
 
@@ -299,6 +352,17 @@ def tile_recurrentsig_kernel(
             bias_ps = psum_acc.tile([P, HALF], F32, tag="acc")
             nc.tensor.matmul(out=bias_ps[:], lhsT=ones[:], rhs=bias_rows[:, cols], start=True, stop=True)
             nc.vector.tensor_copy(out=bias[:, cols], in_=bias_ps[:])
+        bias_cols = const.tile([P, UNITS // P], F32)
+        cols_ps = psum_back.tile([P, HALF], F32, tag="back", name="cols_ps")
+        for chunk in range(UNITS // P):
+            nc.tensor.matmul(
+                out=cols_ps[:, chunk : chunk + 1],
+                lhsT=bias_rows[:, chunk * P : (chunk + 1) * P],
+                rhs=ones[:, 0:1],
+                start=True,
+                stop=True,
+            )
+        nc.scalar.copy(out=bias_cols[:], in_=cols_ps[:, 0 : UNITS // P])
         for planes in plane_sets:
             nc.vector.tensor_copy(out=planes[:, 1, :], in_=tl[:, 0:1].to_broadcast([P, HALF]))
 
@@ -306,27 +370,40 @@ def tile_recurrentsig_kernel(
             for run in range(RUNS):
                 passes(i, run)
         for step in range(STEPS):
-            plane_step(0, step)
+            for lo in range(0, QUARTER, QUARTER // 2):
+                plane_step(0, step, lo, lo + QUARTER // 2)
 
-        turns = {(1, 3): [(2, 0)], (2, 0): [(2, 1)], (2, 1): [(2, 2)], (5, 2): [(3, 0)], (5, 3): [(3, 1)], (6, 0): [(3, 2)]}
-        quants = {(2, 1): (2, 0), (2, 2): (2, 1), (2, 3): (2, 2), (6, 0): (3, 0), (6, 1): (3, 1), (6, 2): (3, 2)}
+        turns = {(1, 3): [(2, 0)], (2, 0): [(2, 1)], (2, 1): [(2, 2)], (4, 3): [(3, 0)], (5, 0): [(3, 1)], (5, 1): [(3, 2)]}
+        quants = {(2, 1): (2, 0), (2, 2): (2, 1), (2, 3): (2, 2), (5, 1): (3, 0), (5, 2): (3, 1), (5, 3): (3, 2)}
         for i in range(len(cells)):
             for step in range(STEPS):
-                for bt, run in turns.get((i, step), []):
+                turns_here = turns.get((i, step), [])
+                for bt, run in turns_here:
                     turn(bt, run)
                 if (i, step) in quants:
                     quantise(*quants[i, step])
+                back_here = step == 0 and i + 1 < len(cells) and is_turned(i + 1)
+                if back_here and turns_here:
+                    turn_back(i + 1)
                 if i == 2 and step > 1:
                     passes(4, step - 2)
                 elif i == 3 and step == 0:
                     passes(4, 2)
-                if i != 2 and step > 0 and i + 2 < len(cells):
+                if i + 2 < len(cells) and is_turned(i + 2):
+                    turned_passes(i + 2, step)
+                elif i + 2 in (2, 3, 5) and step > 0:
                     passes(i + 2, step - 1)
+                if back_here and not turns_here:
+                    turn_back(i + 1)
                 if i == 3:
                     join_piece(i, step)
                 if i + 1 < len(cells):
                     plane_step(i + 1, step)
                 if i != 3:
                     join_piece(i, step)
+            if i + 2 < len(cells) and is_turned(i + 2):
+                add_bias(i + 2)
+            if i == 0:
+                load_weight_words(HALF, HALF)
             if i == 2:
                 load_activations(3)

from contextlib import ExitStack

import concourse.mybir as mybir
from concourse.masks import make_identity

F32 = mybir.dt.float32
BF16 = mybir.dt.bfloat16
I32 = mybir.dt.int32
U32 = mybir.dt.uint32
U8 = mybir.dt.uint8
FP8X4 = mybir.dt.float8_e4m3fn_x4
ALU = mybir.AluOpType
FUNC = mybir.ActivationFunctionType

P = 128
BATCH = 512
INPUTS = 512
UNITS = 1024
SIG = 6
K_PASS = 512
K_ALL = UNITS * SIG + UNITS + INPUTS
GROUPS = K_ALL // K_PASS
U_GROUPS = GROUPS - INPUTS // K_PASS
WORDS = K_PASS // 2
TILES = BATCH // P
HALF = 512
HALVES = UNITS // HALF
SIG_GROUPS = HALF * SIG // K_PASS
ROUND = 2
RUN = SIG_GROUPS
RUNS = -(-GROUPS // RUN)
ROUNDS = -(-GROUPS // ROUND)
PLANES_PER_SLOT = 4
QUARTER = UNITS // 4
STEPS = 4
STORE = 128
PAIR = 2

FLOPS = 2 * BATCH * K_ALL * UNITS


def tile_recurrentsig_kernel(
    tc,
    x,
    prev_sigs,
    prev_states,
    W_w_words,
    W_w_scales,
    W_b,
    U_w_words,
    U_w_scales,
    U_b,
    log_timelapse,
    out,
):
    nc = tc.nc
    with ExitStack() as ctx:
        ctx.enter_context(tc.manual_schedule())
        const = ctx.enter_context(tc.tile_pool(name="const", bufs=1))
        sig_pool = ctx.enter_context(tc.tile_pool(name="sig_pool", bufs=TILES * HALVES - 1))
        rest_pool = ctx.enter_context(tc.tile_pool(name="rest_pool", bufs=TILES))
        quant = ctx.enter_context(tc.tile_pool(name="quant", bufs=TILES - 1))
        stage = ctx.enter_context(tc.tile_pool(name="stage", bufs=6))
        small = ctx.enter_context(tc.tile_pool(name="small", bufs=2))
        turned_sums = ctx.enter_context(tc.tile_pool(name="turned_sums", bufs=2))
        raws = ctx.enter_context(tc.tile_pool(name="raws", bufs=5))
        joins = ctx.enter_context(tc.tile_pool(name="joins", bufs=9))
        psum_t = ctx.enter_context(tc.psum_pool(name="psum_t", bufs=4))
        psum_acc = ctx.enter_context(tc.psum_pool(name="psum_acc", bufs=3))
        psum_back = ctx.enter_context(tc.psum_pool(name="psum_back", bufs=1))

        w_words = const.tile([P, GROUPS, UNITS], U32, align_bytes=64)
        w_planes = const.tile([P, PLANES_PER_SLOT, UNITS], U8, align_bytes=64)
        nc.vector.memset(w_planes[:, 0, :].bitcast(I32), 0)
        bias_rows = stage.tile([P, UNITS], BF16, align_bytes=64, tag="stage")
        nc.vector.memset(bias_rows[:].bitcast(I32), 0)
        for slot in range(1, PLANES_PER_SLOT):
            nc.vector.memset(w_planes[:, slot, :].bitcast(I32), 0)
        ones = const.tile([P, P], BF16)
        nc.vector.memset(ones[:], 1.0)
        ident = const.tile([P, P], F32)
        log_tl = const.tile([P, 1], BF16)

        sig_tiles = {}
        rest_tiles = {}

        def load_sigs(bt, half):
            sigs = sig_pool.tile([P, HALF * SIG], BF16, tag="sigs", name="sigs%d_%d" % (bt, half))
            sig_tiles[bt, half] = sigs
            nc.sync.dma_start(
                out=sigs[:], in_=prev_sigs[bt * P : (bt + 1) * P, half * HALF * SIG : (half + 1) * HALF * SIG]
            )

        def load_rest(bt):
            rows = slice(bt * P, (bt + 1) * P)
            rest = rest_pool.tile([P, UNITS + INPUTS], BF16, tag="rest", name="rest%d" % bt)
            rest_tiles[bt] = rest
            nc.sync.dma_start(out=rest[:, 0:UNITS], in_=prev_states[rows, :])
            nc.sync.dma_start(out=rest[:, UNITS : UNITS + INPUTS], in_=x[rows, :])

        def load_activations(bt):
            for half in range(HALVES):
                load_sigs(bt, half)
            load_rest(bt)

        def load_scale_slot(slot, quadrants=(0, 1, 2, 3)):
            first = slot * PLANES_PER_SLOT
            last = min(first + PLANES_PER_SLOT, U_GROUPS)
            for quadrant in quadrants:
                top = 32 * quadrant
                rows = slice(4 * quadrant, 4 * quadrant + 4)
                nc.sync.dma_start(
                    out=w_planes[top : top + 4 * (last - first), slot, :].bitcast(I32),
                    in_=U_w_scales[first:last, rows, :].bitcast(I32),
                )
                if last == U_GROUPS:
                    top_w = top + 4 * (U_GROUPS - first)
                    nc.sync.dma_start(
                        out=w_planes[top_w : top_w + 4, slot, :].bitcast(I32),
                        in_=W_w_scales[0, rows, :].bitcast(I32),
                    )

        def load_weight_words(unit0, units, behind_each_load=lambda run: None):
            cols = slice(unit0, unit0 + units)
            for first in range(0, U_GROUPS, RUN):
                last = min(first + RUN, U_GROUPS)
                nc.sync.dma_start(
                    out=w_words[:, first:last, cols].bitcast(I32),
                    in_=U_w_words[first:last, :, cols, :].rearrange("g p n t -> p g (n t)").bitcast(I32),
                )
                behind_each_load(first // RUN)
            nc.sync.dma_start(
                out=w_words[:, U_GROUPS, cols].bitcast(I32),
                in_=W_w_words[0, :, cols, :].rearrange("p n t -> p (n t)").bitcast(I32),
            )

        make_identity(nc, ident[:])
        nc.gpsimd.dma_start(out=log_tl[:], in_=log_timelapse.partition_broadcast(P))
        nc.gpsimd.dma_start(out=bias_rows[0:1, :], in_=W_b.unsqueeze(0))
        nc.gpsimd.dma_start(out=bias_rows[1:2, :], in_=U_b.unsqueeze(0))

        load_sigs(0, 0)
        load_scale_slot(0)
        load_sigs(0, 1)
        load_rest(0)
        load_scale_slot(1)
        load_sigs(1, 0)
        load_scale_slot(2)
        load_sigs(1, 1)
        load_scale_slot(3, (0, 1))
        load_rest(1)
        load_weight_words(0, QUARTER, lambda run: load_scale_slot(3, (2, 3)) if run == 1 else None)
        load_weight_words(QUARTER, QUARTER)
        load_activations(2)

        a_words = {}
        a_scales = {}

        def group_words(bt, g):
            if g < HALVES * SIG_GROUPS:
                source, local = sig_tiles[bt, g // SIG_GROUPS], g % SIG_GROUPS
            else:
                source, local = rest_tiles[bt], g - HALVES * SIG_GROUPS
            return source[:, local * K_PASS : (local + 1) * K_PASS].bitcast(F32)

        grouped_tiles = {}

        def rounds_of(run):
            end = min((run + 1) * RUN, GROUPS)
            return [(first, min(ROUND, end - first)) for first in range(run * RUN, end, ROUND)]

        def turn(bt, run):
            for first, count in rounds_of(run):
                turned = psum_t.tile([P, ROUND, 2, P], F32, tag="turned")
                for i in range(count):
                    words = group_words(bt, first + i)
                    for u in range(2):
                        nc.tensor.transpose(turned[:, i, u, :], words[:, u:WORDS:2], ident[:])
                grouped = stage.tile([P, ROUND * K_PASS], BF16, align_bytes=64, tag="stage")
                grouped_tiles[bt, first] = grouped
                nc.scalar.copy(
                    out=grouped[:, 0 : count * K_PASS].bitcast(F32).rearrange("p (g b u) -> p g b u", g=count, u=2),
                    in_=turned[:, 0:count].rearrange("p g u b -> p g b u"),
                )

        def quantise(bt, run):
            if run == 0:
                a_words[bt] = quant.tile([P, GROUPS, P], U32, align_bytes=64, tag="a_words", name="a_words%d" % bt)
                a_scales[bt] = quant.tile([P, GROUPS, P], U8, align_bytes=64, tag="a_scales", name="a_scales%d" % bt)
            for first, count in rounds_of(run):
                nc.vector.quantize_mx(
                    out=a_words[bt][:, first : first + count, :].rearrange("p g b -> p (g b)").bitcast(FP8X4),
                    scales=a_scales[bt][:, first : first + count, :].rearrange("p g b -> p (g b)"),
                    in_=grouped_tiles[bt, first][:, 0 : count * K_PASS],
                )

        def one_pass(g, out, stationary, moving):
            nc.tensor.matmul_mx(
                out=out,
                lhsT=stationary[0],
                lhsT_scale=stationary[1],
                rhs=moving[0],
                rhs_scale=moving[1],
                start=(g == 0),
                stop=(g == GROUPS - 1),
            )

        def weights_of(g, cols):
            planes = w_planes[4 * (g % PLANES_PER_SLOT) : P, g // PLANES_PER_SLOT, cols]
            return w_words[:, g, cols].bitcast(FP8X4), planes

        def codes_of(bt, g):
            return a_words[bt][:, g, :].bitcast(FP8X4), a_scales[bt][:, g, :]

        def passes(i, run):
            bt, unit0, units = cells[i]
            cols = slice(unit0, unit0 + units)
            if run == 0:
                accs[i] = psum_acc.tile([P, HALF], F32, tag="acc", name="acc%d" % i)
            for g in range(run * RUN, min((run + 1) * RUN, GROUPS)):
                one_pass(g, accs[i][:, 0:units], codes_of(bt, g), weights_of(g, cols))

        def turned_passes(i, chunk):
            bt, unit0, units = cells[i]
            cols = slice(unit0 + chunk * P, unit0 + (chunk + 1) * P)
            if chunk == 0:
                accs[i] = psum_acc.tile([P, HALF], F32, tag="acc", name="acc%d" % i)
            for g in range(GROUPS):
                out_cols = accs[i][:, chunk * P : (chunk + 1) * P]
                one_pass(g, out_cols, weights_of(g, cols), codes_of(bt, g))

        def add_bias(i):
            bt, unit0, units = cells[i]
            with_bias[i] = turned_sums.tile([P, HALF], F32, tag="with_bias", name="with_bias%d" % i)
            for chunk in range(HALF // P):
                cols = slice(chunk * P, (chunk + 1) * P)
                at = unit0 // P + chunk
                nc.scalar.activation(
                    out=with_bias[i][:, cols],
                    in_=accs[i][:, cols],
                    func=FUNC.Identity,
                    bias=bias_cols[:, at : at + 1],
                    scale=1.0,
                )

        def turn_back(i):
            accs[i] = psum_back.tile([P, HALF], F32, tag="back", name="back%d" % i)
            for chunk in range(HALF // P):
                cols = slice(chunk * P, (chunk + 1) * P)
                nc.tensor.transpose(accs[i][:, cols], with_bias[i][:, cols], ident[:])

        with_bias = {}

        plane_sets = [const.tile([P, SIG, HALF], F32, name="planes%d" % s) for s in range(2)]

        cell_tiles = {}

        def is_turned(i):
            return i > 5

        def store_raw(i, raw, unit0, units):
            bt = cells[i][0]
            first_col = UNITS * SIG + unit0
            nc.sync.dma_start(out=out[bt * P : (bt + 1) * P, first_col : first_col + units], in_=raw)

        def plane_step(i, step, lo=0, hi=None):
            bt, unit0, units = cells[i]
            units = (hi or units) - lo
            unit0 += lo
            half, u = divmod(unit0, HALF)
            planes = plane_sets[i % 2][:, :, lo : lo + units]
            if step == 0 and lo == 0:
                a0 = small.tile([P, HALF], BF16)
                c = small.tile([P, 2, HALF], F32)
                raw = raws.tile([P, HALF], F32)
                cell_tiles[i] = (a0, c, raw)
            a0, c, raw = (
                cell_tiles[i][0][:, lo : lo + units],
                cell_tiles[i][1][:, :, lo : lo + units],
                cell_tiles[i][2][:, lo : lo + units],
            )
            if step == 0:
                by_unit = sig_tiles[bt, half][:, u * SIG : (u + units) * SIG].rearrange("p (n j) -> p n j", j=SIG)
                nc.scalar.copy(out=a0, in_=by_unit[:, :, 0])
                nc.scalar.activation(
                    out=c[:, 1, :], in_=by_unit[:, :, 1], func=FUNC.Identity, bias=half_tl[:, 0:1], scale=1.0
                )
                if not is_turned(i):
                    nc.vector.tensor_tensor(
                        out=raw, in0=accs[i][:, lo : lo + units], in1=bias[:, unit0 : unit0 + units], op=ALU.add
                    )
                    if lo + units == cells[i][2]:
                        store_raw(i, cell_tiles[i][2][:, 0 : cells[i][2]], cells[i][1], cells[i][2])
            if step == 1:
                states = rest_tiles[bt][:, unit0 : unit0 + units]
                exact = accs[i][:, 0:units] if is_turned(i) else raw
                nc.vector.tensor_tensor(out=planes[:, 0, :], in0=exact, in1=states, op=ALU.subtract)
                if is_turned(i):
                    nc.scalar.copy(out=raw, in_=accs[i][:, 0:units])
                    store_raw(i, raw, unit0, units)
            if step == 2:
                nc.vector.scalar_tensor_tensor(
                    out=c[:, 0, :], in0=planes[:, 0, :], scalar=0.5, in1=a0, op0=ALU.mult, op1=ALU.add
                )
                nc.scalar.activation(out=planes[:, 3:6:2, :], in_=c, func=FUNC.Copy, scale=tl[:, 0:1])
            if step == 3:
                nc.vector.tensor_tensor(
                    out=planes[:, 2:5:2, :],
                    in0=c,
                    in1=planes[:, 0:1, :].to_broadcast([P, 2, units]),
                    op=ALU.mult,
                )

        joined_tiles = {}

        def join_piece(i, piece):
            bt, unit0, units = cells[i]
            half, u = divmod(unit0, HALF)
            count = units // STEPS
            n0 = piece * count
            at = n0 % STORE
            if at == 0:
                joined_tiles[i] = joins.tile([P, STORE * SIG], F32, tag="joined", name="joined%d_%d" % (i, piece))
            joined = joined_tiles[i]
            nc.vector.tensor_tensor(
                out=joined[:, at * SIG : (at + count) * SIG].rearrange("p (m r j) -> p m j r", r=PAIR, j=SIG),
                in0=plane_sets[i % 2][:, :, n0 : n0 + count].rearrange("p j (m r) -> p m j r", r=PAIR),
                in1=sig_tiles[bt, half][:, (u + n0) * SIG : (u + n0 + count) * SIG].rearrange(
                    "p (m r j) -> p m j r", r=PAIR, j=SIG
                ),
                op=ALU.add,
            )
            if at + count == STORE:
                first_col = (unit0 + n0 + count - STORE) * SIG
                nc.sync.dma_start(out=out[bt * P : (bt + 1) * P, first_col : first_col + STORE * SIG], in_=joined[:])

        cells = [(bt, unit0, QUARTER) for unit0 in (0, QUARTER) for bt in (0, 1)]
        cells += [(2, 0, HALF), (0, HALF, HALF), (1, HALF, HALF), (2, HALF, HALF), (3, 0, HALF), (3, HALF, HALF)]
        accs = {}

        for bt in (0, 1):
            for run in range(RUNS):
                turn(bt, run)
                quantise(bt, run)
        tl = const.tile([P, 1], F32)
        nc.scalar.activation(out=tl[:], in_=log_tl[:], func=FUNC.Exp)
        half_tl = const.tile([P, 1], F32)
        nc.scalar.mul(out=half_tl[:], in_=tl[:], mul=0.5)
        bias = const.tile([P, UNITS], F32)
        for half in range(HALVES):
            cols = slice(half * HALF, (half + 1) * HALF)
            bias_ps = psum_acc.tile([P, HALF], F32, tag="acc")
            nc.tensor.matmul(out=bias_ps[:], lhsT=ones[:], rhs=bias_rows[:, cols], start=True, stop=True)
            nc.vector.tensor_copy(out=bias[:, cols], in_=bias_ps[:])
        bias_cols = const.tile([P, UNITS // P], F32)
        cols_ps = psum_back.tile([P, HALF], F32, tag="back", name="cols_ps")
        for chunk in range(UNITS // P):
            nc.tensor.matmul(
                out=cols_ps[:, chunk : chunk + 1],
                lhsT=bias_rows[:, chunk * P : (chunk + 1) * P],
                rhs=ones[:, 0:1],
                start=True,
                stop=True,
            )
        nc.scalar.copy(out=bias_cols[:], in_=cols_ps[:, 0 : UNITS // P])
        for planes in plane_sets:
            nc.vector.tensor_copy(out=planes[:, 1, :], in_=tl[:, 0:1].to_broadcast([P, HALF]))

        for i in (0, 1):
            for run in range(RUNS):
                passes(i, run)
        for step in range(STEPS):
            for lo in range(0, QUARTER, QUARTER // 2):
                plane_step(0, step, lo, lo + QUARTER // 2)

        turns = {(1, 3): [(2, 0)], (2, 0): [(2, 1)], (2, 1): [(2, 2)], (4, 3): [(3, 0)], (5, 0): [(3, 1)], (5, 1): [(3, 2)]}
        quants = {(2, 1): (2, 0), (2, 2): (2, 1), (2, 3): (2, 2), (5, 1): (3, 0), (5, 2): (3, 1), (5, 3): (3, 2)}
        for i in range(len(cells)):
            for step in range(STEPS):
                turns_here = turns.get((i, step), [])
                for bt, run in turns_here:
                    turn(bt, run)
                if (i, step) in quants:
                    quantise(*quants[i, step])
                back_here = step == 0 and i + 1 < len(cells) and is_turned(i + 1)
                if back_here and turns_here:
                    turn_back(i + 1)
                if i == 2 and step > 1:
                    passes(4, step - 2)
                elif i == 3 and step == 0:
                    passes(4, 2)
                if i + 2 < len(cells) and is_turned(i + 2):
                    turned_passes(i + 2, step)
                elif i + 2 in (2, 3, 5) and step > 0:
                    passes(i + 2, step - 1)
                if back_here and not turns_here:
                    turn_back(i + 1)
                if i == 3:
                    join_piece(i, step)
                if i + 1 < len(cells):
                    plane_step(i + 1, step)
                if i != 3:
                    join_piece(i, step)
            if i + 2 < len(cells) and is_turned(i + 2):
                add_bias(i + 2)
            if i == 0:
                load_weight_words(HALF, HALF)
            if i == 2:
                load_activations(3)
